import numpy as np
import ml_dtypes


def mxq(x, axis, fmt="e4m3"):
    dtype, down = {"e4m3": (ml_dtypes.float8_e4m3fn, 7), "e5m2": (ml_dtypes.float8_e5m2, 14)}[fmt]
    v = np.moveaxis(np.asarray(x, np.float32).astype(ml_dtypes.bfloat16).astype(np.float64), axis, -1)
    blocks = v.reshape(v.shape[:-1] + (-1, 32))
    amax = np.abs(blocks).max(-1, keepdims=True)
    byte = np.maximum(np.where(amax > 0, np.frexp(amax)[1] - 1 + 127, 0) - down, 1)
    scale = np.exp2(byte - 127.0)
    codes = (blocks / scale).astype(np.float32).astype(dtype).astype(np.float64)
    return np.moveaxis((codes * scale).reshape(v.shape), -1, axis)


WIDE = False


def mx_kscale(k):
    if not WIDE:
        return np.ones(k)
    levels = np.array([10, -10, 5, -5, 0])
    a = np.random.permutation(np.resize(levels, k // 512 * 4)).reshape(k // 512, 4)
    idx = np.arange(k)
    return np.exp2(a[idx // 512, idx % 128 // 32])


BF16 = ml_dtypes.bfloat16


def bf(x):
    return np.asarray(x, np.float32).astype(BF16)


def f64(x):
    return np.asarray(x).astype(np.float64)


E2M1 = np.array([0.0, 0.5, 1.0, 1.5, 2.0, 3.0, 4.0, 6.0, -0.0, -0.5, -1.0, -1.5, -2.0, -3.0, -4.0, -6.0])


def pack_weight(w, fmt):
    k, n = w.shape
    w = f64(bf(w)).reshape(k // 32, 32, n)
    amax = np.abs(w).max(1)
    if fmt == "e4m3":
        byte = np.frexp(amax)[1] - 1 + 127 - 7
    else:
        mant, ex = np.frexp(amax / 6.0)
        byte = np.where(mant > 0.5, ex, ex - 1) + 127
    byte = np.clip(np.where(amax > 0, byte, 1), 1, 254)
    scaled = (w * np.exp2(127.0 - byte)[:, None, :]).reshape(k, n).astype(np.float32)
    by_word = np.ascontiguousarray(scaled.reshape(k // 512, 128, 4, n).transpose(0, 1, 3, 2))
    if fmt == "e4m3":
        words = by_word.astype(ml_dtypes.float8_e4m3fn).view(np.uint8)
    else:
        c = by_word.astype(ml_dtypes.float4_e2m1fn).view(np.uint8) & 0xF
        words = c[..., 0::2] | (c[..., 1::2] << 4)
    return np.ascontiguousarray(words), np.ascontiguousarray(byte.astype(np.uint8).reshape(k // 512, 16, n))


def unpack_weight(words, scales, fmt):
    g, p, n, _ = words.shape
    if fmt == "e4m3":
        vals = np.ascontiguousarray(words).view(ml_dtypes.float8_e4m3fn).astype(np.float64)
    else:
        nib = np.empty((g, p, n, 4), np.uint8)
        nib[..., 0::2] = words & 0xF
        nib[..., 1::2] = words >> 4
        vals = E2M1[nib]
    vals = vals * np.repeat(np.exp2(scales.astype(np.float64) - 127.0), 8, axis=1)[..., None]
    return vals.transpose(0, 1, 3, 2).reshape(g * 512, n)


N, RANK, H, W, B = 4, 512, 16, 32, 4096
S = H * W
EPS = 1e-5
XS = 0.01


def setup_inputs():
    t = mx_kscale(RANK)
    U = np.random.standard_normal((N, S, RANK)) * 0.5 / np.sqrt(S)
    U[0] = U[0] * t
    x = bf((np.random.standard_normal((B, 1, H, W)) + 0.5) * XS)
    C = np.random.standard_normal((S, RANK)) / np.sqrt(RANK) / t
    C_words, C_scales = pack_weight(np.ascontiguousarray(C.T), "e4m3")
    return {"x": x,
            "U": bf(U),
            "C_words": C_words,
            "C_scales": C_scales,
            "beta": bf(np.random.standard_normal(S) * 0.5),
            "gamma": bf(1.25 + 0.1 * np.random.standard_normal(1)),
            "bn_bias": bf(0.3 + 0.05 * np.random.standard_normal(1))}


def reference(x, U, C_words, C_scales, beta, gamma, bn_bias):
    x = f64(x)
    b = x.shape[0]
    mean = x.mean(axis=(0, 2, 3), keepdims=True)
    var = x.var(axis=(0, 2, 3), keepdims=True)
    xn = (x - mean) * (1.0 / np.sqrt(var + EPS))
    xn = xn * f64(gamma).reshape(1, -1, 1, 1) + f64(bn_bias).reshape(1, -1, 1, 1)
    z = xn.reshape(b, S)
    t = mxq(z, 1, "e4m3") @ mxq(f64(U), 1, "e4m3")
    h = t[0]
    for n in range(1, N):
        h = t[n] * h + h
    out = (mxq(h, 1, "e4m3") @ unpack_weight(C_words, C_scales, "e4m3")) + f64(beta)
    return out.reshape(b, 1, H, W)

@@ -1,0 +1,297 @@
+import concourse.mybir as mybir
+from concourse.masks import make_identity
+
+F32 = mybir.dt.float32
+BF16 = mybir.dt.bfloat16
+I32 = mybir.dt.int32
+U32 = mybir.dt.uint32
+U8 = mybir.dt.uint8
+FP8X4 = mybir.dt.float8_e4m3fn_x4
+ALU = mybir.AluOpType
+ACT = mybir.ActivationFunctionType
+
+P = 128
+PACK = 4
+DEGREE = 4
+BATCH = 4096
+PIXELS = 512
+RANK = 512
+BLOCKS = BATCH // P
+EPS = 1e-5
+X_CHUNK = 4
+X_CHUNKS = BLOCKS // X_CHUNK
+HALF = BLOCKS // 2
+
+FLOPS = 2 * BATCH * PIXELS * RANK * (DEGREE + 1)
+
+
+def tile_generator_pa_t_kernel(tc, x, U, C_words, C_scales, beta, gamma, bn_bias, out):
+    nc = tc.nc
+    x_view = x.rearrange("(p i) c h w -> p i (c h w)", i=BLOCKS)
+    out_view = out.rearrange("(p i) c h w -> p i (c h w)", i=BLOCKS)
+
+    with (
+        tc.tile_pool(name="keep", bufs=1) as keep,
+        tc.tile_pool(name="small", bufs=1) as small,
+        tc.tile_pool(name="stage", bufs=2) as stage,
+        tc.tile_pool(name="work", bufs=3) as work,
+        tc.psum_pool(name="xt_banks", bufs=2) as xt_banks,
+        tc.psum_pool(name="t_banks", bufs=1) as t_banks,
+        tc.psum_pool(name="o_banks", bufs=2) as o_banks,
+    ):
+        x_sb = keep.tile([P, BLOCKS, PIXELS], BF16, name="x_sb")
+        u_raw = keep.tile([P, DEGREE, PACK, RANK], BF16, name="u_raw")
+        gamma_sb = small.tile([P, 1], BF16, name="gamma_sb")
+        bias_sb = small.tile([P, 1], BF16, name="bias_sb")
+        nc.scalar.dma_start(out=gamma_sb[:], in_=gamma.partition_broadcast(P))
+        nc.scalar.dma_start(out=bias_sb[:], in_=bn_bias.partition_broadcast(P))
+
+        def load_u(n):
+            nc.sync.dma_start(
+                out=u_raw[:, n].rearrange("p (u e) r -> p u e r", u=2),
+                in_=U[n].rearrange("(u p e) r -> p u e r", u=2, e=2),
+            )
+
+        for c in range(X_CHUNKS):
+            blocks = slice(c * X_CHUNK, (c + 1) * X_CHUNK)
+            nc.sync.dma_start(out=x_sb[:, blocks, :], in_=x_view[:, blocks, :])
+            if c in (1, 3):
+                load_u(c // 2)
+        load_u(2)
+        load_u(3)
+        w_codes = keep.tile([P, PIXELS], U32, name="w_codes", align_bytes=64)
+        w_scales = keep.tile([P, PIXELS], U8, name="w_scales", align_bytes=64)
+        nc.vector.memset(w_scales[:].bitcast(I32), 0)
+        nc.sync.dma_start(
+            out=w_codes[:].bitcast(I32),
+            in_=C_words[0].rearrange("p n t -> p (n t)").bitcast(I32),
+        )
+        for quadrant in range(4):
+            nc.sync.dma_start(
+                out=w_scales[32 * quadrant : 32 * quadrant + 4, :].bitcast(I32),
+                in_=C_scales[0, 4 * quadrant : 4 * quadrant + 4, :].bitcast(I32),
+            )
+        beta_bc = keep.tile([P, PIXELS], BF16, name="beta_bc")
+        nc.sync.dma_start(out=beta_bc[:], in_=beta.partition_broadcast(P))
+
+        ident = keep.tile([P, P], F32, name="ident")
+        make_identity(nc, ident[:])
+        ones = keep.tile([P, P], BF16, name="ones")
+        nc.vector.memset(ones[:], 1.0)
+        weigh_mean = keep.tile([P, P], F32, name="weigh_mean")
+        nc.vector.memset(weigh_mean[:], 1.0 / (2 * P))
+        weigh_sum = keep.tile([P, P], F32, name="weigh_sum")
+        nc.vector.memset(weigh_sum[:], 1.0 / (BATCH * PIXELS))
+        one = small.tile([P, 1], F32, name="one")
+        nc.vector.memset(one[:], 1.0)
+        warm = small.tile([P, 1], F32, name="warm")
+        nc.scalar.activation(out=warm[:], in_=one[:], func=ACT.Abs_reciprocal_sqrt)
+
+        xT = keep.tile([P, BLOCKS, P, PACK], BF16, name="xT", align_bytes=64)
+        z_codes = keep.tile([P, BLOCKS, P], U32, name="z_codes", align_bytes=64)
+        z_scales = keep.tile([P, BLOCKS, P], U8, name="z_scales", align_bytes=64)
+        u_codes = keep.tile([P, DEGREE, PACK, P], U32, name="u_codes", align_bytes=64)
+        u_scales = keep.tile([P, DEGREE, PACK, P], U8, name="u_scales", align_bytes=64)
+
+        def transpose_chunk(c):
+            for first in range(c * X_CHUNK, (c + 1) * X_CHUNK, 2):
+                xt = xt_banks.tile([P, 2, 2, P], F32, name="xt")
+                for k in range(2):
+                    words = x_sb[:, first + k, :].bitcast(F32)
+                    for u in range(2):
+                        nc.tensor.transpose(xt[:, k, u, :], words[:, u * P : (u + 1) * P], ident[:])
+                nc.scalar.copy(
+                    out=xT[:, first : first + 2, :, :].bitcast(F32),
+                    in_=xt[:].rearrange("p k u b -> p k b u"),
+                )
+
+        stats = small.tile([P, HALF, 6], F32, name="stats")
+        squares = small.tile([P, HALF], F32, name="squares")
+        unread = keep.tile([P, HALF + 1, PIXELS], BF16, name="unread")
+        column_sums = o_banks.tile([P, PIXELS], F32, name="column_sums", tag="o")
+        for pair in range(HALF):
+            even, odd = 2 * pair, 2 * pair + 1
+            nc.vector.bn_stats(out=stats[:, pair, :], in_=x_sb[:, even, :])
+            nc.scalar.activation(
+                out=unread[:, pair, :],
+                in_=x_sb[:, odd, :],
+                func=ACT.Square,
+                accum_out=squares[:, pair : pair + 1],
+            )
+            nc.tensor.matmul(
+                out=column_sums[:],
+                lhsT=ones[:],
+                rhs=x_sb[:, odd, :],
+                start=(pair == 0),
+                stop=(pair == HALF - 1),
+            )
+
+        for n in range(DEGREE):
+            u_grouped = stage.tile([P, PACK, P, PACK], BF16, name="u_grouped", align_bytes=64)
+            nc.gpsimd.tensor_scalar(
+                out=u_grouped[:],
+                in0=u_raw[:, n].rearrange("p t (q j) -> p j q t", j=PACK),
+                scalar1=1.0,
+                scalar2=0.0,
+                op0=ALU.mult,
+                op1=ALU.add,
+            )
+            nc.vector.quantize_mx(
+                out=u_codes[:, n].rearrange("p j q -> p (j q)").bitcast(FP8X4),
+                scales=u_scales[:, n].rearrange("p j q -> p (j q)"),
+                in_=u_grouped[:].rearrange("p j q t -> p (j q t)"),
+            )
+
+        moments_even = small.tile([P, 2], F32, name="moments_even")
+        nc.vector.bn_aggr(out=moments_even[:], in_=stats[:].rearrange("p a s -> p (a s)"))
+        nc.vector.scalar_tensor_tensor(
+            out=moments_even[:, 1:2],
+            in0=moments_even[:, 0:1],
+            scalar=moments_even[:, 0:1],
+            in1=moments_even[:, 1:2],
+            op0=ALU.mult,
+            op1=ALU.add,
+        )
+        sums_odd = small.tile([P, 2], F32, name="sums_odd")
+        nc.scalar.activation(
+            out=unread[:, HALF, :],
+            in_=column_sums[:],
+            func=ACT.Copy,
+            scale=1.0 / P,
+            accum_out=sums_odd[:, 0:1],
+        )
+        unread_squares = small.tile([P, HALF], F32, name="unread_squares")
+        nc.scalar.activation(
+            out=unread_squares[:], in_=squares[:], func=ACT.Copy, accum_out=sums_odd[:, 1:2]
+        )
+        transpose_chunk(0)
+        total = o_banks.tile([P, 2], F32, name="total", tag="o")
+        nc.tensor.matmul(out=total[:], lhsT=weigh_mean[:], rhs=moments_even[:], start=True, stop=False)
+        nc.tensor.matmul(out=total[:], lhsT=weigh_sum[:], rhs=sums_odd[:], start=False, stop=True)
+        moments = small.tile([P, 2], F32, name="moments")
+        nc.vector.tensor_copy(out=moments[:], in_=total[:])
+        mean = moments[:, 0:1]
+        minus_var = small.tile([P, 1], F32, name="minus_var")
+        nc.vector.scalar_tensor_tensor(
+            out=minus_var[:], in0=mean, scalar=mean, in1=moments[:, 1:2], op0=ALU.mult, op1=ALU.subtract
+        )
+        rough = small.tile([P, 1], F32, name="rough")
+        nc.scalar.activation(
+            out=rough[:], in_=minus_var[:], func=ACT.Abs_reciprocal_sqrt, scale=-1.0, bias=EPS
+        )
+        var_eps = small.tile([P, 1], F32, name="var_eps")
+        nc.vector.tensor_scalar(
+            out=var_eps[:], in0=minus_var[:], scalar1=-1.0, scalar2=EPS, op0=ALU.mult, op1=ALU.add
+        )
+        minus_mean = small.tile([P, 1], F32, name="minus_mean")
+        nc.vector.tensor_scalar(out=minus_mean[:], in0=mean, scalar1=-1.0, scalar2=None, op0=ALU.mult)
+        newton = small.tile([P, 1], F32, name="newton")
+        nc.vector.scalar_tensor_tensor(
+            out=newton[:], in0=var_eps[:], scalar=rough[:], in1=rough[:], op0=ALU.mult, op1=ALU.mult
+        )
+        nc.vector.tensor_scalar(
+            out=newton[:], in0=newton[:], scalar1=-0.5, scalar2=1.5, op0=ALU.mult, op1=ALU.add
+        )
+        scale_a = small.tile([P, 1], F32, name="scale_a")
+        shift_b = small.tile([P, 1], F32, name="shift_b")
+        nc.vector.scalar_tensor_tensor(
+            out=scale_a[:], in0=rough[:], scalar=newton[:], in1=gamma_sb[:], op0=ALU.mult, op1=ALU.mult
+        )
+        nc.vector.scalar_tensor_tensor(
+            out=shift_b[:], in0=minus_mean[:], scalar=scale_a[:], in1=bias_sb[:], op0=ALU.mult, op1=ALU.add
+        )
+
+        h_bf16 = {}
+        o_psum = {}
+        o_sb = {}
+
+        def normalise_and_quantise(c):
+            blocks = slice(c * X_CHUNK, (c + 1) * X_CHUNK)
+            z = stage.tile([P, X_CHUNK * P * PACK], BF16, name="z", align_bytes=64)
+            nc.vector.tensor_scalar(
+                out=z[:],
+                in0=xT[:, blocks].rearrange("p i b t -> p (i b t)"),
+                scalar1=scale_a[:],
+                scalar2=shift_b[:],
+                op0=ALU.mult,
+                op1=ALU.add,
+            )
+            nc.vector.quantize_mx(
+                out=z_codes[:, blocks].rearrange("p i b -> p (i b)").bitcast(FP8X4),
+                scales=z_scales[:, blocks].rearrange("p i b -> p (i b)"),
+                in_=z[:],
+            )
+
+        def first_stage(i):
+            t = []
+            for n in range(DEGREE):
+                bank = t_banks.tile([P, PACK, P], F32, name="t%d" % n)
+                for j in range(PACK):
+                    nc.tensor.matmul_mx(
+                        out=bank[:, j, :],
+                        lhsT=u_codes[:, n, j, :].bitcast(FP8X4),
+                        lhsT_scale=u_scales[:, n, j, :],
+                        rhs=z_codes[:, i, :].bitcast(FP8X4),
+                        rhs_scale=z_scales[:, i, :],
+                        start=True,
+                        stop=True,
+                    )
+                t.append(bank[:].rearrange("p j b -> p b j"))
+            left = work.tile([P, P, PACK], F32, name="left")
+            right = work.tile([P, P, PACK], F32, name="right")
+            nc.scalar.copy(out=left[:], in_=t[0])
+            nc.scalar.activation(out=right[:], in_=t[2], func=ACT.Identity, bias=1.0)
+            nc.vector.scalar_tensor_tensor(
+                out=left[:], in0=t[1], scalar=1.0, in1=left[:], op0=ALU.add, op1=ALU.mult
+            )
+            nc.vector.scalar_tensor_tensor(
+                out=right[:], in0=t[3], scalar=1.0, in1=right[:], op0=ALU.add, op1=ALU.mult
+            )
+            h_bf16[i] = work.tile([P, P, PACK], BF16, name="h_bf16", align_bytes=64)
+            nc.gpsimd.tensor_tensor(out=h_bf16[i][:], in0=left[:], in1=right[:], op=ALU.mult)
+
+        def second_stage(i):
+            h_codes = work.tile([P, P], U32, name="h_codes", align_bytes=64)
+            h_scales = work.tile([P, P], U8, name="h_scales", align_bytes=64)
+            nc.vector.quantize_mx(
+                out=h_codes[:].bitcast(FP8X4),
+                scales=h_scales[:],
+                in_=h_bf16[i][:].rearrange("p b j -> p (b j)"),
+            )
+            o_psum[i] = o_banks.tile([P, PIXELS], F32, name="o_psum", tag="o")
+            nc.tensor.matmul_mx(
+                out=o_psum[i][:],
+                lhsT=h_codes[:].bitcast(FP8X4),
+                lhsT_scale=h_scales[:],
+                rhs=w_codes[:].bitcast(FP8X4),
+                rhs_scale=w_scales[:],
+                start=True,
+                stop=True,
+            )
+
+        def add_beta_and_store(i):
+            if i % 2 == 0:
+                o_sb[i // 2] = work.tile([P, 2, PIXELS], F32, name="o_sb")
+                nc.vector.tensor_tensor(
+                    out=o_sb[i // 2][:, 0, :], in0=o_psum[i][:], in1=beta_bc[:], op=ALU.add
+                )
+            else:
+                odd_rows = o_sb[i // 2][:, 1, :]
+                nc.scalar.copy(out=odd_rows, in_=o_psum[i][:])
+                nc.gpsimd.tensor_tensor(out=odd_rows, in0=odd_rows, in1=beta_bc[:], op=ALU.add)
+                nc.sync.dma_start(out=out_view[:, i - 1 : i + 1, :], in_=o_sb[i // 2][:])
+
+        transpose_chunk(1)
+        normalise_and_quantise(0)
+        for i in range(BLOCKS + 2):
+            if i < BLOCKS:
+                first_stage(i)
+                c = i // X_CHUNK
+                if i % X_CHUNK == 0 and c + 2 < X_CHUNKS:
+                    transpose_chunk(c + 2)
+                if i % X_CHUNK == 0 and c + 1 < X_CHUNKS:
+                    normalise_and_quantise(c + 1)
+            if 0 <= i - 1 < BLOCKS:
+                second_stage(i - 1)
+            if 0 <= i - 2:
+                add_beta_and_store(i - 2)

@@ -21,6 +21,10 @@ EPS = 1e-5
 X_CHUNK = 4
 X_CHUNKS = BLOCKS // X_CHUNK
 HALF = BLOCKS // 2
+AHEAD = 8
+QUANT_LAG = 1
+W_LAG = 2
+OUT_LAG = 3
 
 FLOPS = 2 * BATCH * PIXELS * RANK * (DEGREE + 1)
 
@@ -34,10 +38,12 @@ def tile_generator_pa_t_kernel(tc, x, U, C_words, C_scales, beta, gamma, bn_bias
         tc.tile_pool(name="keep", bufs=1) as keep,
         tc.tile_pool(name="small", bufs=1) as small,
         tc.tile_pool(name="stage", bufs=2) as stage,
-        tc.tile_pool(name="work", bufs=3) as work,
-        tc.psum_pool(name="xt_banks", bufs=2) as xt_banks,
-        tc.psum_pool(name="t_banks", bufs=1) as t_banks,
+        tc.tile_pool(name="work", bufs=4) as work,
+        tc.psum_pool(name="xt_banks", bufs=1) as xt_banks,
+        tc.psum_pool(name="s_banks", bufs=1) as s_banks,
+        tc.psum_pool(name="v_banks", bufs=4) as v_banks,
         tc.psum_pool(name="o_banks", bufs=2) as o_banks,
+        tc.manual_schedule(),
     ):
         x_sb = keep.tile([P, BLOCKS, PIXELS], BF16, name="x_sb")
         u_raw = keep.tile([P, DEGREE, PACK, RANK], BF16, name="u_raw")
@@ -93,17 +99,39 @@ def tile_generator_pa_t_kernel(tc, x, U, C_words, C_scales, beta, gamma, bn_bias
         u_codes = keep.tile([P, DEGREE, PACK, P], U32, name="u_codes", align_bytes=64)
         u_scales = keep.tile([P, DEGREE, PACK, P], U8, name="u_scales", align_bytes=64)
 
-        def transpose_chunk(c):
-            for first in range(c * X_CHUNK, (c + 1) * X_CHUNK, 2):
-                xt = xt_banks.tile([P, 2, 2, P], F32, name="xt")
-                for k in range(2):
-                    words = x_sb[:, first + k, :].bitcast(F32)
-                    for u in range(2):
-                        nc.tensor.transpose(xt[:, k, u, :], words[:, u * P : (u + 1) * P], ident[:])
-                nc.scalar.copy(
-                    out=xT[:, first : first + 2, :, :].bitcast(F32),
-                    in_=xt[:].rearrange("p k u b -> p k b u"),
-                )
+        def transpose_pair(pair):
+            xt = xt_banks.tile([P, 2, 2, P], F32, name="xt")
+            for k in range(2):
+                words = x_sb[:, 2 * pair + k, :].bitcast(F32)
+                for u in range(2):
+                    nc.tensor.transpose(xt[:, k, u, :], words[:, u * P : (u + 1) * P], ident[:])
+            nc.scalar.copy(
+                out=xT[:, 2 * pair : 2 * pair + 2, :, :].bitcast(F32),
+                in_=xt[:].rearrange("p k u b -> p k b u"),
+            )
+
+        u_grouped = {}
+
+        def regroup_u(n):
+            u_grouped[n] = keep.tile([P, PACK, P, PACK], BF16, name="u_grouped%d" % n, align_bytes=64)
+            nc.gpsimd.tensor_scalar(
+                out=u_grouped[n][:],
+                in0=u_raw[:, n].rearrange("p t (q j) -> p j q t", j=PACK),
+                scalar1=1.0,
+                scalar2=0.0,
+                op0=ALU.mult,
+                op1=ALU.add,
+            )
+
+        def quantise_u(n):
+            nc.vector.quantize_mx(
+                out=u_codes[:, n].rearrange("p j q -> p (j q)").bitcast(FP8X4),
+                scales=u_scales[:, n].rearrange("p j q -> p (j q)"),
+                in_=u_grouped[n][:].rearrange("p j q t -> p (j q t)"),
+            )
+
+        for n in range(DEGREE):
+            regroup_u(n)
 
         stats = small.tile([P, HALF, 6], F32, name="stats")
         squares = small.tile([P, HALF], F32, name="squares")
@@ -124,22 +152,6 @@ def tile_generator_pa_t_kernel(tc, x, U, C_words, C_scales, beta, gamma, bn_bias
                 rhs=x_sb[:, odd, :],
                 start=(pair == 0),
                 stop=(pair == HALF - 1),
-            )
-
-        for n in range(DEGREE):
-            u_grouped = stage.tile([P, PACK, P, PACK], BF16, name="u_grouped", align_bytes=64)
-            nc.gpsimd.tensor_scalar(
-                out=u_grouped[:],
-                in0=u_raw[:, n].rearrange("p t (q j) -> p j q t", j=PACK),
-                scalar1=1.0,
-                scalar2=0.0,
-                op0=ALU.mult,
-                op1=ALU.add,
-            )
-            nc.vector.quantize_mx(
-                out=u_codes[:, n].rearrange("p j q -> p (j q)").bitcast(FP8X4),
-                scales=u_scales[:, n].rearrange("p j q -> p (j q)"),
-                in_=u_grouped[:].rearrange("p j q t -> p (j q t)"),
             )
 
         moments_even = small.tile([P, 2], F32, name="moments_even")
@@ -164,7 +176,8 @@ def tile_generator_pa_t_kernel(tc, x, U, C_words, C_scales, beta, gamma, bn_bias
         nc.scalar.activation(
             out=unread_squares[:], in_=squares[:], func=ACT.Copy, accum_out=sums_odd[:, 1:2]
         )
-        transpose_chunk(0)
+        transpose_pair(0)
+        quantise_u(0)
         total = o_banks.tile([P, 2], F32, name="total", tag="o")
         nc.tensor.matmul(out=total[:], lhsT=weigh_mean[:], rhs=moments_even[:], start=True, stop=False)
         nc.tensor.matmul(out=total[:], lhsT=weigh_sum[:], rhs=sums_odd[:], start=False, stop=True)
@@ -185,6 +198,7 @@ def tile_generator_pa_t_kernel(tc, x, U, C_words, C_scales, beta, gamma, bn_bias
         )
         minus_mean = small.tile([P, 1], F32, name="minus_mean")
         nc.vector.tensor_scalar(out=minus_mean[:], in0=mean, scalar1=-1.0, scalar2=None, op0=ALU.mult)
+        quantise_u(1)
         newton = small.tile([P, 1], F32, name="newton")
         nc.vector.scalar_tensor_tensor(
             out=newton[:], in0=var_eps[:], scalar=rough[:], in1=rough[:], op0=ALU.mult, op1=ALU.mult
@@ -200,10 +214,6 @@ def tile_generator_pa_t_kernel(tc, x, U, C_words, C_scales, beta, gamma, bn_bias
         nc.vector.scalar_tensor_tensor(
             out=shift_b[:], in0=minus_mean[:], scalar=scale_a[:], in1=bias_sb[:], op0=ALU.mult, op1=ALU.add
         )
-
-        h_bf16 = {}
-        o_psum = {}
-        o_sb = {}
 
         def normalise_and_quantise(c):
             blocks = slice(c * X_CHUNK, (c + 1) * X_CHUNK)
@@ -222,10 +232,18 @@ def tile_generator_pa_t_kernel(tc, x, U, C_words, C_scales, beta, gamma, bn_bias
                 in_=z[:],
             )
 
+        t_psum = {}
+        product = {}
+        h_bf16 = {}
+        h_codes = {}
+        h_scales = {}
+        o_psum = {}
+        o_sb = {}
+
         def first_stage(i):
-            t = []
             for n in range(DEGREE):
-                bank = t_banks.tile([P, PACK, P], F32, name="t%d" % n)
+                banks = s_banks if n == 0 else v_banks
+                bank = banks.tile([P, PACK, P], F32, name="t")
                 for j in range(PACK):
                     nc.tensor.matmul_mx(
                         out=bank[:, j, :],
@@ -236,33 +254,35 @@ def tile_generator_pa_t_kernel(tc, x, U, C_words, C_scales, beta, gamma, bn_bias
                         start=True,
                         stop=True,
                     )
-                t.append(bank[:].rearrange("p j b -> p b j"))
-            left = work.tile([P, P, PACK], F32, name="left")
-            right = work.tile([P, P, PACK], F32, name="right")
-            nc.scalar.copy(out=left[:], in_=t[0])
-            nc.scalar.activation(out=right[:], in_=t[2], func=ACT.Identity, bias=1.0)
-            nc.vector.scalar_tensor_tensor(
-                out=left[:], in0=t[1], scalar=1.0, in1=left[:], op0=ALU.add, op1=ALU.mult
-            )
-            nc.vector.scalar_tensor_tensor(
-                out=right[:], in0=t[3], scalar=1.0, in1=right[:], op0=ALU.add, op1=ALU.mult
-            )
-            h_bf16[i] = work.tile([P, P, PACK], BF16, name="h_bf16", align_bytes=64)
-            nc.gpsimd.tensor_tensor(out=h_bf16[i][:], in0=left[:], in1=right[:], op=ALU.mult)
+                t_psum[i, n] = bank[:].rearrange("p j b -> p b j")
+            product[i] = work.tile([P, P, PACK], F32, name="product")
+            nc.scalar.copy(out=product[i][:], in_=t_psum[i, 0])
 
-        def second_stage(i):
-            h_codes = work.tile([P, P], U32, name="h_codes", align_bytes=64)
-            h_scales = work.tile([P, P], U8, name="h_scales", align_bytes=64)
+        def multiply_by_factor(i, n):
+            if n < DEGREE - 1:
+                result = product[i]
+            else:
+                h_bf16[i] = work.tile([P, P, PACK], BF16, name="h_bf16", align_bytes=64)
+                result = h_bf16[i]
+            nc.vector.scalar_tensor_tensor(
+                out=result[:], in0=t_psum[i, n], scalar=1.0, in1=product[i][:], op0=ALU.add, op1=ALU.mult
+            )
+
+        def quantise_h(i):
+            h_codes[i] = work.tile([P, P], U32, name="h_codes", align_bytes=64)
+            h_scales[i] = work.tile([P, P], U8, name="h_scales", align_bytes=64)
             nc.vector.quantize_mx(
-                out=h_codes[:].bitcast(FP8X4),
-                scales=h_scales[:],
+                out=h_codes[i][:].bitcast(FP8X4),
+                scales=h_scales[i][:],
                 in_=h_bf16[i][:].rearrange("p b j -> p (b j)"),
             )
+
+        def second_stage(i):
             o_psum[i] = o_banks.tile([P, PIXELS], F32, name="o_psum", tag="o")
             nc.tensor.matmul_mx(
                 out=o_psum[i][:],
-                lhsT=h_codes[:].bitcast(FP8X4),
-                lhsT_scale=h_scales[:],
+                lhsT=h_codes[i][:].bitcast(FP8X4),
+                lhsT_scale=h_scales[i][:],
                 rhs=w_codes[:].bitcast(FP8X4),
                 rhs_scale=w_scales[:],
                 start=True,
@@ -272,26 +292,35 @@ def tile_generator_pa_t_kernel(tc, x, U, C_words, C_scales, beta, gamma, bn_bias
         def add_beta_and_store(i):
             if i % 2 == 0:
                 o_sb[i // 2] = work.tile([P, 2, PIXELS], F32, name="o_sb")
-                nc.vector.tensor_tensor(
-                    out=o_sb[i // 2][:, 0, :], in0=o_psum[i][:], in1=beta_bc[:], op=ALU.add
-                )
-            else:
-                odd_rows = o_sb[i // 2][:, 1, :]
-                nc.scalar.copy(out=odd_rows, in_=o_psum[i][:])
-                nc.gpsimd.tensor_tensor(out=odd_rows, in0=odd_rows, in1=beta_bc[:], op=ALU.add)
+            nc.vector.tensor_tensor(
+                out=o_sb[i // 2][:, i % 2, :], in0=o_psum[i][:], in1=beta_bc[:], op=ALU.add
+            )
+            if i % 2 == 1:
                 nc.sync.dma_start(out=out_view[:, i - 1 : i + 1, :], in_=o_sb[i // 2][:])
 
-        transpose_chunk(1)
+        for pair in range(1, AHEAD // 2):
+            transpose_pair(pair)
         normalise_and_quantise(0)
-        for i in range(BLOCKS + 2):
+        quantise_u(2)
+        normalise_and_quantise(1)
+        quantise_u(3)
+        first_stage(0)
+        for i in range(BLOCKS + OUT_LAG):
             if i < BLOCKS:
-                first_stage(i)
-                c = i // X_CHUNK
-                if i % X_CHUNK == 0 and c + 2 < X_CHUNKS:
-                    transpose_chunk(c + 2)
-                if i % X_CHUNK == 0 and c + 1 < X_CHUNKS:
-                    normalise_and_quantise(c + 1)
-            if 0 <= i - 1 < BLOCKS:
-                second_stage(i - 1)
-            if 0 <= i - 2:
-                add_beta_and_store(i - 2)
+                multiply_by_factor(i, 1)
+            if 0 <= i - QUANT_LAG < BLOCKS:
+                quantise_h(i - QUANT_LAG)
+            if i < BLOCKS:
+                multiply_by_factor(i, 2)
+            if 0 <= i - OUT_LAG:
+                add_beta_and_store(i - OUT_LAG)
+            if i < BLOCKS:
+                multiply_by_factor(i, 3)
+            if i + 1 < BLOCKS:
+                first_stage(i + 1)
+            if 0 <= i - W_LAG < BLOCKS:
+                second_stage(i - W_LAG)
+            if i % 2 == 0 and i + AHEAD < BLOCKS:
+                transpose_pair((i + AHEAD) // 2)
+            if i % X_CHUNK == X_CHUNK - 1 and i + 1 + X_CHUNK < BLOCKS:
+                normalise_and_quantise((i + 1) // X_CHUNK + 1)

@@ -292,9 +292,9 @@ def tile_generator_pa_t_kernel(tc, x, U, C_words, C_scales, beta, gamma, bn_bias
         def add_beta_and_store(i):
             if i % 2 == 0:
                 o_sb[i // 2] = work.tile([P, 2, PIXELS], F32, name="o_sb")
-            nc.vector.tensor_tensor(
-                out=o_sb[i // 2][:, i % 2, :], in0=o_psum[i][:], in1=beta_bc[:], op=ALU.add
-            )
+            rows = o_sb[i // 2][:, i % 2, :]
+            nc.scalar.copy(out=rows, in_=o_psum[i][:])
+            nc.gpsimd.tensor_tensor(out=rows, in0=rows, in1=beta_bc[:], op=ALU.add)
             if i % 2 == 1:
                 nc.sync.dma_start(out=out_view[:, i - 1 : i + 1, :], in_=o_sb[i // 2][:])
 

@@ -22,9 +22,9 @@ X_CHUNK = 4
 X_CHUNKS = BLOCKS // X_CHUNK
 HALF = BLOCKS // 2
 AHEAD = 8
-QUANT_LAG = 1
-W_LAG = 2
-OUT_LAG = 3
+QUANT_LAG = 2
+W_LAG = 3
+OUT_LAG = 4
 
 FLOPS = 2 * BATCH * PIXELS * RANK * (DEGREE + 1)
 
@@ -40,8 +40,8 @@ def tile_generator_pa_t_kernel(tc, x, U, C_words, C_scales, beta, gamma, bn_bias
         tc.tile_pool(name="stage", bufs=2) as stage,
         tc.tile_pool(name="work", bufs=4) as work,
         tc.psum_pool(name="xt_banks", bufs=1) as xt_banks,
-        tc.psum_pool(name="s_banks", bufs=1) as s_banks,
-        tc.psum_pool(name="v_banks", bufs=4) as v_banks,
+        tc.psum_pool(name="s_banks", bufs=2) as s_banks,
+        tc.psum_pool(name="v_banks", bufs=3) as v_banks,
         tc.psum_pool(name="o_banks", bufs=2) as o_banks,
         tc.manual_schedule(),
     ):
@@ -233,7 +233,8 @@ def tile_generator_pa_t_kernel(tc, x, U, C_words, C_scales, beta, gamma, bn_bias
             )
 
         t_psum = {}
-        product = {}
+        left = {}
+        right = {}
         h_bf16 = {}
         h_codes = {}
         h_scales = {}
@@ -242,7 +243,7 @@ def tile_generator_pa_t_kernel(tc, x, U, C_words, C_scales, beta, gamma, bn_bias
 
         def first_stage(i):
             for n in range(DEGREE):
-                banks = s_banks if n == 0 else v_banks
+                banks = s_banks if n % 2 == 0 else v_banks
                 bank = banks.tile([P, PACK, P], F32, name="t")
                 for j in range(PACK):
                     nc.tensor.matmul_mx(
@@ -255,18 +256,20 @@ def tile_generator_pa_t_kernel(tc, x, U, C_words, C_scales, beta, gamma, bn_bias
                         stop=True,
                     )
                 t_psum[i, n] = bank[:].rearrange("p j b -> p b j")
-            product[i] = work.tile([P, P, PACK], F32, name="product")
-            nc.scalar.copy(out=product[i][:], in_=t_psum[i, 0])
+            left[i] = work.tile([P, P, PACK], F32, name="left")
+            right[i] = work.tile([P, P, PACK], F32, name="right")
+            nc.scalar.copy(out=left[i][:], in_=t_psum[i, 0])
+            nc.scalar.activation(out=right[i][:], in_=t_psum[i, 2], func=ACT.Identity, bias=1.0)
 
-        def multiply_by_factor(i, n):
-            if n < DEGREE - 1:
-                result = product[i]
-            else:
-                h_bf16[i] = work.tile([P, P, PACK], BF16, name="h_bf16", align_bytes=64)
-                result = h_bf16[i]
+        def multiply_factors(i):
             nc.vector.scalar_tensor_tensor(
-                out=result[:], in0=t_psum[i, n], scalar=1.0, in1=product[i][:], op0=ALU.add, op1=ALU.mult
+                out=left[i][:], in0=t_psum[i, 1], scalar=1.0, in1=left[i][:], op0=ALU.add, op1=ALU.mult
             )
+            nc.vector.scalar_tensor_tensor(
+                out=right[i][:], in0=t_psum[i, 3], scalar=1.0, in1=right[i][:], op0=ALU.add, op1=ALU.mult
+            )
+            h_bf16[i] = work.tile([P, P, PACK], BF16, name="h_bf16", align_bytes=64)
+            nc.gpsimd.tensor_tensor(out=h_bf16[i][:], in0=left[i][:], in1=right[i][:], op=ALU.mult)
 
         def quantise_h(i):
             h_codes[i] = work.tile([P, P], U32, name="h_codes", align_bytes=64)
@@ -292,9 +295,9 @@ def tile_generator_pa_t_kernel(tc, x, U, C_words, C_scales, beta, gamma, bn_bias
         def add_beta_and_store(i):
             if i % 2 == 0:
                 o_sb[i // 2] = work.tile([P, 2, PIXELS], F32, name="o_sb")
-            rows = o_sb[i // 2][:, i % 2, :]
-            nc.scalar.copy(out=rows, in_=o_psum[i][:])
-            nc.gpsimd.tensor_tensor(out=rows, in0=rows, in1=beta_bc[:], op=ALU.add)
+            nc.vector.tensor_tensor(
+                out=o_sb[i // 2][:, i % 2, :], in0=o_psum[i][:], in1=beta_bc[:], op=ALU.add
+            )
             if i % 2 == 1:
                 nc.sync.dma_start(out=out_view[:, i - 1 : i + 1, :], in_=o_sb[i // 2][:])
 
@@ -307,20 +310,16 @@ def tile_generator_pa_t_kernel(tc, x, U, C_words, C_scales, beta, gamma, bn_bias
         first_stage(0)
         for i in range(BLOCKS + OUT_LAG):
             if i < BLOCKS:
-                multiply_by_factor(i, 1)
-            if 0 <= i - QUANT_LAG < BLOCKS:
-                quantise_h(i - QUANT_LAG)
-            if i < BLOCKS:
-                multiply_by_factor(i, 2)
-            if 0 <= i - OUT_LAG:
-                add_beta_and_store(i - OUT_LAG)
-            if i < BLOCKS:
-                multiply_by_factor(i, 3)
+                multiply_factors(i)
             if i + 1 < BLOCKS:
                 first_stage(i + 1)
             if 0 <= i - W_LAG < BLOCKS:
                 second_stage(i - W_LAG)
             if i % 2 == 0 and i + AHEAD < BLOCKS:
                 transpose_pair((i + AHEAD) // 2)
+            if 0 <= i - QUANT_LAG < BLOCKS:
+                quantise_h(i - QUANT_LAG)
+            if 0 <= i - OUT_LAG:
+                add_beta_and_store(i - OUT_LAG)
             if i % X_CHUNK == X_CHUNK - 1 and i + 1 + X_CHUNK < BLOCKS:
                 normalise_and_quantise((i + 1) // X_CHUNK + 1)

@@ -295,10 +295,13 @@ def tile_generator_pa_t_kernel(tc, x, U, C_words, C_scales, beta, gamma, bn_bias
         def add_beta_and_store(i):
             if i % 2 == 0:
                 o_sb[i // 2] = work.tile([P, 2, PIXELS], F32, name="o_sb")
-            nc.vector.tensor_tensor(
-                out=o_sb[i // 2][:, i % 2, :], in0=o_psum[i][:], in1=beta_bc[:], op=ALU.add
-            )
-            if i % 2 == 1:
+                even_rows = o_sb[i // 2][:, 0, :]
+                nc.scalar.copy(out=even_rows, in_=o_psum[i][:])
+                nc.gpsimd.tensor_tensor(out=even_rows, in0=even_rows, in1=beta_bc[:], op=ALU.add)
+            else:
+                nc.vector.tensor_tensor(
+                    out=o_sb[i // 2][:, 1, :], in0=o_psum[i][:], in1=beta_bc[:], op=ALU.add
+                )
                 nc.sync.dma_start(out=out_view[:, i - 1 : i + 1, :], in_=o_sb[i // 2][:])
 
         for pair in range(1, AHEAD // 2):

@@ -20,8 +20,8 @@ BLOCKS = BATCH // P
 EPS = 1e-5
 X_CHUNK = 4
 X_CHUNKS = BLOCKS // X_CHUNK
-HALF = BLOCKS // 2
 AHEAD = 8
+Z_AHEAD = 6
 QUANT_LAG = 2
 W_LAG = 3
 OUT_LAG = 4
@@ -133,54 +133,57 @@ def tile_generator_pa_t_kernel(tc, x, U, C_words, C_scales, beta, gamma, bn_bias
         for n in range(DEGREE):
             regroup_u(n)
 
-        stats = small.tile([P, HALF, 6], F32, name="stats")
-        squares = small.tile([P, HALF], F32, name="squares")
-        unread = keep.tile([P, HALF + 1, PIXELS], BF16, name="unread")
+        stats = small.tile([P, X_CHUNKS, 2, 6], F32, name="stats")
+        squares = small.tile([P, X_CHUNKS], F32, name="squares")
+        unread = keep.tile([P, X_CHUNKS, 2, PIXELS], BF16, name="unread")
         column_sums = o_banks.tile([P, PIXELS], F32, name="column_sums", tag="o")
-        for pair in range(HALF):
-            even, odd = 2 * pair, 2 * pair + 1
-            nc.vector.bn_stats(out=stats[:, pair, :], in_=x_sb[:, even, :])
+        for c in range(X_CHUNKS):
+            first = c * X_CHUNK
+            for k in range(2):
+                nc.vector.bn_stats(out=stats[:, c, k, :], in_=x_sb[:, first + k, :])
             nc.scalar.activation(
-                out=unread[:, pair, :],
-                in_=x_sb[:, odd, :],
+                out=unread[:, c],
+                in_=x_sb[:, first + 2 : first + 4, :],
                 func=ACT.Square,
-                accum_out=squares[:, pair : pair + 1],
+                accum_out=squares[:, c : c + 1],
             )
-            nc.tensor.matmul(
-                out=column_sums[:],
-                lhsT=ones[:],
-                rhs=x_sb[:, odd, :],
-                start=(pair == 0),
-                stop=(pair == HALF - 1),
-            )
+            for k in range(2, 4):
+                nc.tensor.matmul(
+                    out=column_sums[:],
+                    lhsT=ones[:],
+                    rhs=x_sb[:, first + k, :],
+                    start=(c == 0 and k == 2),
+                    stop=(c == X_CHUNKS - 1 and k == 3),
+                )
 
-        moments_even = small.tile([P, 2], F32, name="moments_even")
-        nc.vector.bn_aggr(out=moments_even[:], in_=stats[:].rearrange("p a s -> p (a s)"))
+        moments_part = small.tile([P, 2], F32, name="moments_part")
+        nc.vector.bn_aggr(out=moments_part[:], in_=stats[:].rearrange("p c k s -> p (c k s)"))
         nc.vector.scalar_tensor_tensor(
-            out=moments_even[:, 1:2],
-            in0=moments_even[:, 0:1],
-            scalar=moments_even[:, 0:1],
-            in1=moments_even[:, 1:2],
+            out=moments_part[:, 1:2],
+            in0=moments_part[:, 0:1],
+            scalar=moments_part[:, 0:1],
+            in1=moments_part[:, 1:2],
             op0=ALU.mult,
             op1=ALU.add,
         )
-        sums_odd = small.tile([P, 2], F32, name="sums_odd")
+        sums_part = small.tile([P, 2], F32, name="sums_part")
+        unread_sums = keep.tile([P, PIXELS], BF16, name="unread_sums")
         nc.scalar.activation(
-            out=unread[:, HALF, :],
+            out=unread_sums[:],
             in_=column_sums[:],
             func=ACT.Copy,
             scale=1.0 / P,
-            accum_out=sums_odd[:, 0:1],
+            accum_out=sums_part[:, 0:1],
         )
-        unread_squares = small.tile([P, HALF], F32, name="unread_squares")
+        unread_squares = small.tile([P, X_CHUNKS], F32, name="unread_squares")
         nc.scalar.activation(
-            out=unread_squares[:], in_=squares[:], func=ACT.Copy, accum_out=sums_odd[:, 1:2]
+            out=unread_squares[:], in_=squares[:], func=ACT.Copy, accum_out=sums_part[:, 1:2]
         )
         transpose_pair(0)
         quantise_u(0)
         total = o_banks.tile([P, 2], F32, name="total", tag="o")
-        nc.tensor.matmul(out=total[:], lhsT=weigh_mean[:], rhs=moments_even[:], start=True, stop=False)
-        nc.tensor.matmul(out=total[:], lhsT=weigh_sum[:], rhs=sums_odd[:], start=False, stop=True)
+        nc.tensor.matmul(out=total[:], lhsT=weigh_mean[:], rhs=moments_part[:], start=True, stop=False)
+        nc.tensor.matmul(out=total[:], lhsT=weigh_sum[:], rhs=sums_part[:], start=False, stop=True)
         moments = small.tile([P, 2], F32, name="moments")
         nc.vector.tensor_copy(out=moments[:], in_=total[:])
         mean = moments[:, 0:1]
@@ -192,44 +195,51 @@ def tile_generator_pa_t_kernel(tc, x, U, C_words, C_scales, beta, gamma, bn_bias
         nc.scalar.activation(
             out=rough[:], in_=minus_var[:], func=ACT.Abs_reciprocal_sqrt, scale=-1.0, bias=EPS
         )
-        var_eps = small.tile([P, 1], F32, name="var_eps")
+        minus_half_v = small.tile([P, 1], F32, name="minus_half_v")
         nc.vector.tensor_scalar(
-            out=var_eps[:], in0=minus_var[:], scalar1=-1.0, scalar2=EPS, op0=ALU.mult, op1=ALU.add
+            out=minus_half_v[:], in0=minus_var[:], scalar1=0.5, scalar2=-0.5 * EPS, op0=ALU.mult, op1=ALU.add
         )
         minus_mean = small.tile([P, 1], F32, name="minus_mean")
         nc.vector.tensor_scalar(out=minus_mean[:], in0=mean, scalar1=-1.0, scalar2=None, op0=ALU.mult)
         quantise_u(1)
-        newton = small.tile([P, 1], F32, name="newton")
-        nc.vector.scalar_tensor_tensor(
-            out=newton[:], in0=var_eps[:], scalar=rough[:], in1=rough[:], op0=ALU.mult, op1=ALU.mult
-        )
+        correction = small.tile([P, 1], F32, name="correction")
         nc.vector.tensor_scalar(
-            out=newton[:], in0=newton[:], scalar1=-0.5, scalar2=1.5, op0=ALU.mult, op1=ALU.add
+            out=correction[:], in0=rough[:], scalar1=rough[:], scalar2=minus_half_v[:], op0=ALU.mult, op1=ALU.mult
         )
+        rough_gamma = small.tile([P, 1], F32, name="rough_gamma")
+        nc.vector.tensor_tensor(out=rough_gamma[:], in0=rough[:], in1=gamma_sb[:], op=ALU.mult)
         scale_a = small.tile([P, 1], F32, name="scale_a")
         shift_b = small.tile([P, 1], F32, name="shift_b")
         nc.vector.scalar_tensor_tensor(
-            out=scale_a[:], in0=rough[:], scalar=newton[:], in1=gamma_sb[:], op0=ALU.mult, op1=ALU.mult
+            out=scale_a[:], in0=correction[:], scalar=1.5, in1=rough_gamma[:], op0=ALU.add, op1=ALU.mult
         )
         nc.vector.scalar_tensor_tensor(
             out=shift_b[:], in0=minus_mean[:], scalar=scale_a[:], in1=bias_sb[:], op0=ALU.mult, op1=ALU.add
         )
 
-        def normalise_and_quantise(c):
+        z = {}
+
+        def normalise(engine_is_vector, first, count):
+            c = first // X_CHUNK
+            if first % X_CHUNK == 0:
+                z[c] = stage.tile([P, X_CHUNK, P * PACK], BF16, name="z", align_bytes=64)
+            z_blocks = z[c][:, first % X_CHUNK : first % X_CHUNK + count, :]
+            x_blocks = xT[:, first : first + count].rearrange("p i b t -> p i (b t)")
+            if engine_is_vector:
+                nc.vector.tensor_scalar(
+                    out=z_blocks, in0=x_blocks, scalar1=scale_a[:], scalar2=shift_b[:], op0=ALU.mult, op1=ALU.add
+                )
+            else:
+                nc.scalar.activation(
+                    out=z_blocks, in_=x_blocks, func=ACT.Identity, scale=scale_a[:], bias=shift_b[:]
+                )
+
+        def quantise_z(c):
             blocks = slice(c * X_CHUNK, (c + 1) * X_CHUNK)
-            z = stage.tile([P, X_CHUNK * P * PACK], BF16, name="z", align_bytes=64)
-            nc.vector.tensor_scalar(
-                out=z[:],
-                in0=xT[:, blocks].rearrange("p i b t -> p (i b t)"),
-                scalar1=scale_a[:],
-                scalar2=shift_b[:],
-                op0=ALU.mult,
-                op1=ALU.add,
-            )
             nc.vector.quantize_mx(
                 out=z_codes[:, blocks].rearrange("p i b -> p (i b)").bitcast(FP8X4),
                 scales=z_scales[:, blocks].rearrange("p i b -> p (i b)"),
-                in_=z[:],
+                in_=z[c][:].rearrange("p i e -> p (i e)"),
             )
 
         t_psum = {}
@@ -295,20 +305,19 @@ def tile_generator_pa_t_kernel(tc, x, U, C_words, C_scales, beta, gamma, bn_bias
         def add_beta_and_store(i):
             if i % 2 == 0:
                 o_sb[i // 2] = work.tile([P, 2, PIXELS], F32, name="o_sb")
-                even_rows = o_sb[i // 2][:, 0, :]
-                nc.scalar.copy(out=even_rows, in_=o_psum[i][:])
-                nc.gpsimd.tensor_tensor(out=even_rows, in0=even_rows, in1=beta_bc[:], op=ALU.add)
-            else:
-                nc.vector.tensor_tensor(
-                    out=o_sb[i // 2][:, 1, :], in0=o_psum[i][:], in1=beta_bc[:], op=ALU.add
-                )
+            nc.vector.tensor_tensor(
+                out=o_sb[i // 2][:, i % 2, :], in0=o_psum[i][:], in1=beta_bc[:], op=ALU.add
+            )
+            if i % 2 == 1:
                 nc.sync.dma_start(out=out_view[:, i - 1 : i + 1, :], in_=o_sb[i // 2][:])
 
         for pair in range(1, AHEAD // 2):
             transpose_pair(pair)
-        normalise_and_quantise(0)
+        normalise(True, 0, X_CHUNK)
+        quantise_z(0)
+        for i in range(X_CHUNK, Z_AHEAD):
+            normalise(False, i, 1)
         quantise_u(2)
-        normalise_and_quantise(1)
         quantise_u(3)
         first_stage(0)
         for i in range(BLOCKS + OUT_LAG):
@@ -320,9 +329,11 @@ def tile_generator_pa_t_kernel(tc, x, U, C_words, C_scales, beta, gamma, bn_bias
                 second_stage(i - W_LAG)
             if i % 2 == 0 and i + AHEAD < BLOCKS:
                 transpose_pair((i + AHEAD) // 2)
+            if i + Z_AHEAD < BLOCKS:
+                normalise(False, i + Z_AHEAD, 1)
             if 0 <= i - QUANT_LAG < BLOCKS:
                 quantise_h(i - QUANT_LAG)
             if 0 <= i - OUT_LAG:
                 add_beta_and_store(i - OUT_LAG)
-            if i % X_CHUNK == X_CHUNK - 1 and i + 1 + X_CHUNK < BLOCKS:
-                normalise_and_quantise((i + 1) // X_CHUNK + 1)
+            if (i + Z_AHEAD) % X_CHUNK == 0 and X_CHUNK < i + Z_AHEAD <= BLOCKS:
+                quantise_z((i + Z_AHEAD) // X_CHUNK - 1)

@@ -20,7 +20,7 @@ BLOCKS = BATCH // P
 EPS = 1e-5
 X_CHUNK = 4
 X_CHUNKS = BLOCKS // X_CHUNK
-AHEAD = 8
+VECTOR_BLOCKS = (3, 2)
 Z_AHEAD = 6
 QUANT_LAG = 2
 W_LAG = 3
@@ -39,8 +39,7 @@ def tile_generator_pa_t_kernel(tc, x, U, C_words, C_scales, beta, gamma, bn_bias
         tc.tile_pool(name="small", bufs=1) as small,
         tc.tile_pool(name="stage", bufs=2) as stage,
         tc.tile_pool(name="work", bufs=4) as work,
-        tc.psum_pool(name="xt_banks", bufs=1) as xt_banks,
-        tc.psum_pool(name="s_banks", bufs=2) as s_banks,
+        tc.psum_pool(name="s_banks", bufs=3) as s_banks,
         tc.psum_pool(name="v_banks", bufs=3) as v_banks,
         tc.psum_pool(name="o_banks", bufs=2) as o_banks,
         tc.manual_schedule(),
@@ -82,10 +81,10 @@ def tile_generator_pa_t_kernel(tc, x, U, C_words, C_scales, beta, gamma, bn_bias
 
         ident = keep.tile([P, P], F32, name="ident")
         make_identity(nc, ident[:])
-        ones = keep.tile([P, P], BF16, name="ones")
+        ones = keep.tile([P, 1], BF16, name="ones")
         nc.vector.memset(ones[:], 1.0)
         weigh_mean = keep.tile([P, P], F32, name="weigh_mean")
-        nc.vector.memset(weigh_mean[:], 1.0 / (2 * P))
+        nc.vector.memset(weigh_mean[:], sum(VECTOR_BLOCKS) / (2 * X_CHUNK) / P)
         weigh_sum = keep.tile([P, P], F32, name="weigh_sum")
         nc.vector.memset(weigh_sum[:], 1.0 / (BATCH * PIXELS))
         one = small.tile([P, 1], F32, name="one")
@@ -100,7 +99,7 @@ def tile_generator_pa_t_kernel(tc, x, U, C_words, C_scales, beta, gamma, bn_bias
         u_scales = keep.tile([P, DEGREE, PACK, P], U8, name="u_scales", align_bytes=64)
 
         def transpose_pair(pair):
-            xt = xt_banks.tile([P, 2, 2, P], F32, name="xt")
+            xt = v_banks.tile([P, 2, 2, P], F32, name="xt", tag="v")
             for k in range(2):
                 words = x_sb[:, 2 * pair + k, :].bitcast(F32)
                 for u in range(2):
@@ -109,6 +108,10 @@ def tile_generator_pa_t_kernel(tc, x, U, C_words, C_scales, beta, gamma, bn_bias
                 out=xT[:, 2 * pair : 2 * pair + 2, :, :].bitcast(F32),
                 in_=xt[:].rearrange("p k u b -> p k b u"),
             )
+
+        def transpose_chunk(c):
+            for pair in range(c * X_CHUNK // 2, (c + 1) * X_CHUNK // 2):
+                transpose_pair(pair)
 
         u_grouped = {}
 
@@ -133,31 +136,27 @@ def tile_generator_pa_t_kernel(tc, x, U, C_words, C_scales, beta, gamma, bn_bias
         for n in range(DEGREE):
             regroup_u(n)
 
-        stats = small.tile([P, X_CHUNKS, 2, 6], F32, name="stats")
-        squares = small.tile([P, X_CHUNKS], F32, name="squares")
-        unread = keep.tile([P, X_CHUNKS, 2, PIXELS], BF16, name="unread")
-        column_sums = o_banks.tile([P, PIXELS], F32, name="column_sums", tag="o")
+        vector_blocks = [i for i in range(BLOCKS) if i % X_CHUNK < VECTOR_BLOCKS[i // X_CHUNK % 2]]
+        tensor_blocks = [i for i in range(BLOCKS) if i not in vector_blocks]
+        stats = small.tile([P, len(vector_blocks), 6], F32, name="stats")
+        gram = o_banks.tile([P, P], F32, name="gram", tag="o")
+        column_sums = o_banks.tile([P, 1], F32, name="column_sums", tag="o")
         for c in range(X_CHUNKS):
-            first = c * X_CHUNK
-            for k in range(2):
-                nc.vector.bn_stats(out=stats[:, c, k, :], in_=x_sb[:, first + k, :])
-            nc.scalar.activation(
-                out=unread[:, c],
-                in_=x_sb[:, first + 2 : first + 4, :],
-                func=ACT.Square,
-                accum_out=squares[:, c : c + 1],
-            )
-            for k in range(2, 4):
-                nc.tensor.matmul(
-                    out=column_sums[:],
-                    lhsT=ones[:],
-                    rhs=x_sb[:, first + k, :],
-                    start=(c == 0 and k == 2),
-                    stop=(c == X_CHUNKS - 1 and k == 3),
-                )
+            for i in range(c * X_CHUNK, (c + 1) * X_CHUNK):
+                if i in vector_blocks:
+                    nc.vector.bn_stats(out=stats[:, vector_blocks.index(i), :], in_=x_sb[:, i, :])
+                    continue
+                for q in range(PIXELS // P):
+                    columns = x_sb[:, i, q * P : (q + 1) * P]
+                    first = i == tensor_blocks[0] and q == 0
+                    last = i == tensor_blocks[-1] and q == PIXELS // P - 1
+                    nc.tensor.matmul(out=gram[:], lhsT=columns, rhs=columns, start=first, stop=last)
+                    nc.tensor.matmul(out=column_sums[:], lhsT=columns, rhs=ones[:], start=first, stop=last)
+            if c < X_CHUNKS - 1:
+                transpose_chunk(c)
 
         moments_part = small.tile([P, 2], F32, name="moments_part")
-        nc.vector.bn_aggr(out=moments_part[:], in_=stats[:].rearrange("p c k s -> p (c k s)"))
+        nc.vector.bn_aggr(out=moments_part[:], in_=stats[:].rearrange("p k s -> p (k s)"))
         nc.vector.scalar_tensor_tensor(
             out=moments_part[:, 1:2],
             in0=moments_part[:, 0:1],
@@ -167,21 +166,19 @@ def tile_generator_pa_t_kernel(tc, x, U, C_words, C_scales, beta, gamma, bn_bias
             op1=ALU.add,
         )
         sums_part = small.tile([P, 2], F32, name="sums_part")
-        unread_sums = keep.tile([P, PIXELS], BF16, name="unread_sums")
-        nc.scalar.activation(
-            out=unread_sums[:],
-            in_=column_sums[:],
-            func=ACT.Copy,
-            scale=1.0 / P,
-            accum_out=sums_part[:, 0:1],
+        unread = keep.tile([P, P], F32, name="unread")
+        nc.vector.scalar_tensor_tensor(
+            out=unread[:],
+            in0=gram[:],
+            scalar=1.0,
+            in1=ident[:],
+            op0=ALU.mult,
+            op1=ALU.mult,
+            accum_out=sums_part[:, 1:2],
         )
-        unread_squares = small.tile([P, X_CHUNKS], F32, name="unread_squares")
-        nc.scalar.activation(
-            out=unread_squares[:], in_=squares[:], func=ACT.Copy, accum_out=sums_part[:, 1:2]
-        )
-        transpose_pair(0)
+        nc.vector.tensor_copy(out=sums_part[:, 0:1], in_=column_sums[:])
         quantise_u(0)
-        total = o_banks.tile([P, 2], F32, name="total", tag="o")
+        total = s_banks.tile([P, 2], F32, name="total", tag="s")
         nc.tensor.matmul(out=total[:], lhsT=weigh_mean[:], rhs=moments_part[:], start=True, stop=False)
         nc.tensor.matmul(out=total[:], lhsT=weigh_sum[:], rhs=sums_part[:], start=False, stop=True)
         moments = small.tile([P, 2], F32, name="moments")
@@ -195,6 +192,7 @@ def tile_generator_pa_t_kernel(tc, x, U, C_words, C_scales, beta, gamma, bn_bias
         nc.scalar.activation(
             out=rough[:], in_=minus_var[:], func=ACT.Abs_reciprocal_sqrt, scale=-1.0, bias=EPS
         )
+        transpose_chunk(X_CHUNKS - 1)
         minus_half_v = small.tile([P, 1], F32, name="minus_half_v")
         nc.vector.tensor_scalar(
             out=minus_half_v[:], in0=minus_var[:], scalar1=0.5, scalar2=-0.5 * EPS, op0=ALU.mult, op1=ALU.add
@@ -253,8 +251,10 @@ def tile_generator_pa_t_kernel(tc, x, U, C_words, C_scales, beta, gamma, bn_bias
 
         def first_stage(i):
             for n in range(DEGREE):
-                banks = s_banks if n % 2 == 0 else v_banks
-                bank = banks.tile([P, PACK, P], F32, name="t")
+                if n % 2 == 0:
+                    bank = s_banks.tile([P, PACK, P], F32, name="s", tag="s")
+                else:
+                    bank = v_banks.tile([P, PACK, P], F32, name="v", tag="v")
                 for j in range(PACK):
                     nc.tensor.matmul_mx(
                         out=bank[:, j, :],
@@ -311,8 +311,6 @@ def tile_generator_pa_t_kernel(tc, x, U, C_words, C_scales, beta, gamma, bn_bias
             if i % 2 == 1:
                 nc.sync.dma_start(out=out_view[:, i - 1 : i + 1, :], in_=o_sb[i // 2][:])
 
-        for pair in range(1, AHEAD // 2):
-            transpose_pair(pair)
         normalise(True, 0, X_CHUNK)
         quantise_z(0)
         for i in range(X_CHUNK, Z_AHEAD):
@@ -327,13 +325,11 @@ def tile_generator_pa_t_kernel(tc, x, U, C_words, C_scales, beta, gamma, bn_bias
                 first_stage(i + 1)
             if 0 <= i - W_LAG < BLOCKS:
                 second_stage(i - W_LAG)
-            if i % 2 == 0 and i + AHEAD < BLOCKS:
-                transpose_pair((i + AHEAD) // 2)
             if i + Z_AHEAD < BLOCKS:
                 normalise(False, i + Z_AHEAD, 1)
             if 0 <= i - QUANT_LAG < BLOCKS:
                 quantise_h(i - QUANT_LAG)
-            if 0 <= i - OUT_LAG:
-                add_beta_and_store(i - OUT_LAG)
             if (i + Z_AHEAD) % X_CHUNK == 0 and X_CHUNK < i + Z_AHEAD <= BLOCKS:
                 quantise_z((i + Z_AHEAD) // X_CHUNK - 1)
+            if 0 <= i - OUT_LAG:
+                add_beta_and_store(i - OUT_LAG)

@@ -21,10 +21,10 @@ EPS = 1e-5
 X_CHUNK = 4
 X_CHUNKS = BLOCKS // X_CHUNK
 VECTOR_BLOCKS = (3, 2)
-Z_AHEAD = 6
-QUANT_LAG = 2
-W_LAG = 3
-OUT_LAG = 4
+Z_AHEAD = 4
+QUANT_LAG = 1
+W_LAG = 2
+OUT_LAG = 3
 
 FLOPS = 2 * BATCH * PIXELS * RANK * (DEGREE + 1)
 
@@ -37,8 +37,8 @@ def tile_generator_pa_t_kernel(tc, x, U, C_words, C_scales, beta, gamma, bn_bias
     with (
         tc.tile_pool(name="keep", bufs=1) as keep,
         tc.tile_pool(name="small", bufs=1) as small,
-        tc.tile_pool(name="stage", bufs=2) as stage,
         tc.tile_pool(name="work", bufs=4) as work,
+        tc.tile_pool(name="codes", bufs=8) as codes_pool,
         tc.psum_pool(name="s_banks", bufs=3) as s_banks,
         tc.psum_pool(name="v_banks", bufs=3) as v_banks,
         tc.psum_pool(name="o_banks", bufs=2) as o_banks,
@@ -93,8 +93,8 @@ def tile_generator_pa_t_kernel(tc, x, U, C_words, C_scales, beta, gamma, bn_bias
         nc.scalar.activation(out=warm[:], in_=one[:], func=ACT.Abs_reciprocal_sqrt)
 
         xT = keep.tile([P, BLOCKS, P, PACK], BF16, name="xT", align_bytes=64)
-        z_codes = keep.tile([P, BLOCKS, P], U32, name="z_codes", align_bytes=64)
-        z_scales = keep.tile([P, BLOCKS, P], U8, name="z_scales", align_bytes=64)
+        z_codes = keep.tile([P, Z_AHEAD, P], U32, name="z_codes", align_bytes=64)
+        z_scales = keep.tile([P, Z_AHEAD, P], U8, name="z_scales", align_bytes=64)
         u_codes = keep.tile([P, DEGREE, PACK, P], U32, name="u_codes", align_bytes=64)
         u_scales = keep.tile([P, DEGREE, PACK, P], U8, name="u_scales", align_bytes=64)
 
@@ -215,13 +215,7 @@ def tile_generator_pa_t_kernel(tc, x, U, C_words, C_scales, beta, gamma, bn_bias
             out=shift_b[:], in0=minus_mean[:], scalar=scale_a[:], in1=bias_sb[:], op0=ALU.mult, op1=ALU.add
         )
 
-        z = {}
-
-        def normalise(engine_is_vector, first, count):
-            c = first // X_CHUNK
-            if first % X_CHUNK == 0:
-                z[c] = stage.tile([P, X_CHUNK, P * PACK], BF16, name="z", align_bytes=64)
-            z_blocks = z[c][:, first % X_CHUNK : first % X_CHUNK + count, :]
+        def normalise(engine_is_vector, z_blocks, first, count):
             x_blocks = xT[:, first : first + count].rearrange("p i b t -> p i (b t)")
             if engine_is_vector:
                 nc.vector.tensor_scalar(
@@ -232,24 +226,17 @@ def tile_generator_pa_t_kernel(tc, x, U, C_words, C_scales, beta, gamma, bn_bias
                     out=z_blocks, in_=x_blocks, func=ACT.Identity, scale=scale_a[:], bias=shift_b[:]
                 )
 
-        def quantise_z(c):
-            blocks = slice(c * X_CHUNK, (c + 1) * X_CHUNK)
-            nc.vector.quantize_mx(
-                out=z_codes[:, blocks].rearrange("p i b -> p (i b)").bitcast(FP8X4),
-                scales=z_scales[:, blocks].rearrange("p i b -> p (i b)"),
-                in_=z[c][:].rearrange("p i e -> p (i e)"),
-            )
-
+        z_operand = {}
         t_psum = {}
         left = {}
         right = {}
-        h_bf16 = {}
-        h_codes = {}
-        h_scales = {}
+        hz = {}
+        h_operand = {}
         o_psum = {}
         o_sb = {}
 
         def first_stage(i):
+            codes, scales = z_operand[i]
             for n in range(DEGREE):
                 if n % 2 == 0:
                     bank = s_banks.tile([P, PACK, P], F32, name="s", tag="s")
@@ -260,8 +247,8 @@ def tile_generator_pa_t_kernel(tc, x, U, C_words, C_scales, beta, gamma, bn_bias
                         out=bank[:, j, :],
                         lhsT=u_codes[:, n, j, :].bitcast(FP8X4),
                         lhsT_scale=u_scales[:, n, j, :],
-                        rhs=z_codes[:, i, :].bitcast(FP8X4),
-                        rhs_scale=z_scales[:, i, :],
+                        rhs=codes.bitcast(FP8X4),
+                        rhs_scale=scales,
                         start=True,
                         stop=True,
                     )
@@ -278,24 +265,34 @@ def tile_generator_pa_t_kernel(tc, x, U, C_words, C_scales, beta, gamma, bn_bias
             nc.vector.scalar_tensor_tensor(
                 out=right[i][:], in0=t_psum[i, 3], scalar=1.0, in1=right[i][:], op0=ALU.add, op1=ALU.mult
             )
-            h_bf16[i] = work.tile([P, P, PACK], BF16, name="h_bf16", align_bytes=64)
-            nc.gpsimd.tensor_tensor(out=h_bf16[i][:], in0=left[i][:], in1=right[i][:], op=ALU.mult)
-
-        def quantise_h(i):
-            h_codes[i] = work.tile([P, P], U32, name="h_codes", align_bytes=64)
-            h_scales[i] = work.tile([P, P], U8, name="h_scales", align_bytes=64)
-            nc.vector.quantize_mx(
-                out=h_codes[i][:].bitcast(FP8X4),
-                scales=h_scales[i][:],
-                in_=h_bf16[i][:].rearrange("p b j -> p (b j)"),
+            hz[i] = work.tile([P, 2, P * PACK], BF16, name="hz", align_bytes=64)
+            nc.gpsimd.tensor_tensor(
+                out=hz[i][:, 0, :],
+                in0=left[i][:].rearrange("p b j -> p (b j)"),
+                in1=right[i][:].rearrange("p b j -> p (b j)"),
+                op=ALU.mult,
             )
 
+        def quantise(i):
+            count = 2 if i + Z_AHEAD < BLOCKS else 1
+            codes = codes_pool.tile([P, 2, P], U32, name="hz_codes", align_bytes=64)
+            scales = codes_pool.tile([P, 2, P], U8, name="hz_scales", align_bytes=64)
+            nc.vector.quantize_mx(
+                out=codes[:, :count].rearrange("p k b -> p (k b)").bitcast(FP8X4),
+                scales=scales[:, :count].rearrange("p k b -> p (k b)"),
+                in_=hz[i][:, :count].rearrange("p k e -> p (k e)"),
+            )
+            h_operand[i] = codes[:, 0, :], scales[:, 0, :]
+            if count == 2:
+                z_operand[i + Z_AHEAD] = codes[:, 1, :], scales[:, 1, :]
+
         def second_stage(i):
+            codes, scales = h_operand[i]
             o_psum[i] = o_banks.tile([P, PIXELS], F32, name="o_psum", tag="o")
             nc.tensor.matmul_mx(
                 out=o_psum[i][:],
-                lhsT=h_codes[i][:].bitcast(FP8X4),
-                lhsT_scale=h_scales[i][:],
+                lhsT=codes.bitcast(FP8X4),
+                lhsT_scale=scales,
                 rhs=w_codes[:].bitcast(FP8X4),
                 rhs_scale=w_scales[:],
                 start=True,
@@ -311,25 +308,28 @@ def tile_generator_pa_t_kernel(tc, x, U, C_words, C_scales, beta, gamma, bn_bias
             if i % 2 == 1:
                 nc.sync.dma_start(out=out_view[:, i - 1 : i + 1, :], in_=o_sb[i // 2][:])
 
-        normalise(True, 0, X_CHUNK)
-        quantise_z(0)
-        for i in range(X_CHUNK, Z_AHEAD):
-            normalise(False, i, 1)
+        z_first = keep.tile([P, Z_AHEAD, P * PACK], BF16, name="z_first", align_bytes=64)
+        normalise(True, z_first[:], 0, Z_AHEAD)
+        nc.vector.quantize_mx(
+            out=z_codes[:].rearrange("p i b -> p (i b)").bitcast(FP8X4),
+            scales=z_scales[:].rearrange("p i b -> p (i b)"),
+            in_=z_first[:].rearrange("p i e -> p (i e)"),
+        )
+        for i in range(Z_AHEAD):
+            z_operand[i] = z_codes[:, i, :], z_scales[:, i, :]
         quantise_u(2)
         quantise_u(3)
         first_stage(0)
         for i in range(BLOCKS + OUT_LAG):
             if i < BLOCKS:
                 multiply_factors(i)
+            if 0 <= i - QUANT_LAG < BLOCKS:
+                quantise(i - QUANT_LAG)
             if i + 1 < BLOCKS:
                 first_stage(i + 1)
             if 0 <= i - W_LAG < BLOCKS:
                 second_stage(i - W_LAG)
             if i + Z_AHEAD < BLOCKS:
-                normalise(False, i + Z_AHEAD, 1)
-            if 0 <= i - QUANT_LAG < BLOCKS:
-                quantise_h(i - QUANT_LAG)
-            if (i + Z_AHEAD) % X_CHUNK == 0 and X_CHUNK < i + Z_AHEAD <= BLOCKS:
-                quantise_z((i + Z_AHEAD) // X_CHUNK - 1)
+                normalise(False, hz[i][:, 1:2, :], i + Z_AHEAD, 1)
             if 0 <= i - OUT_LAG:
                 add_beta_and_store(i - OUT_LAG)

@@ -20,11 +20,15 @@ BLOCKS = BATCH // P
 EPS = 1e-5
 X_CHUNK = 4
 X_CHUNKS = BLOCKS // X_CHUNK
-VECTOR_BLOCKS = (3, 2)
-Z_AHEAD = 4
-QUANT_LAG = 1
-W_LAG = 2
-OUT_LAG = 3
+SQUARE_CHUNKS = 7
+Z_AHEAD = 5
+QUANT_LAG = 2
+W_LAG = 3
+OUT_LAG = 4
+EARLY_CHUNKS = 4
+LATE_PAIRS = 4
+LATE_ROUND = 2
+LATE_STEP = 3
 
 FLOPS = 2 * BATCH * PIXELS * RANK * (DEGREE + 1)
 
@@ -58,12 +62,15 @@ def tile_generator_pa_t_kernel(tc, x, U, C_words, C_scales, beta, gamma, bn_bias
             )
 
         for c in range(X_CHUNKS):
-            blocks = slice(c * X_CHUNK, (c + 1) * X_CHUNK)
-            nc.sync.dma_start(out=x_sb[:, blocks, :], in_=x_view[:, blocks, :])
-            if c in (1, 3):
-                load_u(c // 2)
-        load_u(2)
-        load_u(3)
+            pieces = 2 if c == X_CHUNKS - 1 else 1
+            for k in range(pieces):
+                size = X_CHUNK // pieces
+                blocks = slice(c * X_CHUNK + k * size, c * X_CHUNK + (k + 1) * size)
+                nc.sync.dma_start(out=x_sb[:, blocks, :], in_=x_view[:, blocks, :])
+            if c == 3:
+                load_u(0)
+        for n in range(1, DEGREE):
+            load_u(n)
         w_codes = keep.tile([P, PIXELS], U32, name="w_codes", align_bytes=64)
         w_scales = keep.tile([P, PIXELS], U8, name="w_scales", align_bytes=64)
         nc.vector.memset(w_scales[:].bitcast(I32), 0)
@@ -84,7 +91,7 @@ def tile_generator_pa_t_kernel(tc, x, U, C_words, C_scales, beta, gamma, bn_bias
         ones = keep.tile([P, 1], BF16, name="ones")
         nc.vector.memset(ones[:], 1.0)
         weigh_mean = keep.tile([P, P], F32, name="weigh_mean")
-        nc.vector.memset(weigh_mean[:], sum(VECTOR_BLOCKS) / (2 * X_CHUNK) / P)
+        nc.vector.memset(weigh_mean[:], 1.0 / (2 * P))
         weigh_sum = keep.tile([P, P], F32, name="weigh_sum")
         nc.vector.memset(weigh_sum[:], 1.0 / (BATCH * PIXELS))
         one = small.tile([P, 1], F32, name="one")
@@ -115,16 +122,15 @@ def tile_generator_pa_t_kernel(tc, x, U, C_words, C_scales, beta, gamma, bn_bias
 
         u_grouped = {}
 
-        def regroup_u(n):
+        def regroup_u(n, on_scalar):
             u_grouped[n] = keep.tile([P, PACK, P, PACK], BF16, name="u_grouped%d" % n, align_bytes=64)
-            nc.gpsimd.tensor_scalar(
-                out=u_grouped[n][:],
-                in0=u_raw[:, n].rearrange("p t (q j) -> p j q t", j=PACK),
-                scalar1=1.0,
-                scalar2=0.0,
-                op0=ALU.mult,
-                op1=ALU.add,
-            )
+            raw = u_raw[:, n].rearrange("p t (q j) -> p j q t", j=PACK)
+            if on_scalar:
+                nc.scalar.copy(out=u_grouped[n][:], in_=raw)
+            else:
+                nc.gpsimd.tensor_scalar(
+                    out=u_grouped[n][:], in0=raw, scalar1=1.0, scalar2=0.0, op0=ALU.mult, op1=ALU.add
+                )
 
         def quantise_u(n):
             nc.vector.quantize_mx(
@@ -133,27 +139,41 @@ def tile_generator_pa_t_kernel(tc, x, U, C_words, C_scales, beta, gamma, bn_bias
                 in_=u_grouped[n][:].rearrange("p j q t -> p (j q t)"),
             )
 
-        for n in range(DEGREE):
-            regroup_u(n)
+        for n in range(DEGREE - 1):
+            regroup_u(n, False)
 
-        vector_blocks = [i for i in range(BLOCKS) if i % X_CHUNK < VECTOR_BLOCKS[i // X_CHUNK % 2]]
-        tensor_blocks = [i for i in range(BLOCKS) if i not in vector_blocks]
-        stats = small.tile([P, len(vector_blocks), 6], F32, name="stats")
+        stats = small.tile([P, BLOCKS // 2, 6], F32, name="stats")
+        squares = small.tile([P, SQUARE_CHUNKS], F32, name="squares")
+        unread_x = keep.tile([P, SQUARE_CHUNKS, PIXELS], BF16, name="unread_x")
+        scalar_part = small.tile([P, 2], F32, name="scalar_part")
+        nc.vector.memset(scalar_part[:, 0:1], 0.0)
         gram = o_banks.tile([P, P], F32, name="gram", tag="o")
         column_sums = o_banks.tile([P, 1], F32, name="column_sums", tag="o")
         for c in range(X_CHUNKS):
             for i in range(c * X_CHUNK, (c + 1) * X_CHUNK):
-                if i in vector_blocks:
-                    nc.vector.bn_stats(out=stats[:, vector_blocks.index(i), :], in_=x_sb[:, i, :])
+                if i % 2 == 0:
+                    nc.vector.bn_stats(out=stats[:, i // 2, :], in_=x_sb[:, i, :])
                     continue
+                by_scalar = c < SQUARE_CHUNKS and i % X_CHUNK == X_CHUNK - 1
+                if by_scalar:
+                    nc.scalar.activation(
+                        out=unread_x[:, c],
+                        in_=x_sb[:, i, :],
+                        func=ACT.Square,
+                        accum_out=squares[:, c : c + 1],
+                    )
                 for q in range(PIXELS // P):
                     columns = x_sb[:, i, q * P : (q + 1) * P]
-                    first = i == tensor_blocks[0] and q == 0
-                    last = i == tensor_blocks[-1] and q == PIXELS // P - 1
-                    nc.tensor.matmul(out=gram[:], lhsT=columns, rhs=columns, start=first, stop=last)
+                    first = i == 1 and q == 0
+                    last = i == BLOCKS - 1 and q == PIXELS // P - 1
+                    if not by_scalar:
+                        nc.tensor.matmul(out=gram[:], lhsT=columns, rhs=columns, start=first, stop=last)
                     nc.tensor.matmul(out=column_sums[:], lhsT=columns, rhs=ones[:], start=first, stop=last)
-            if c < X_CHUNKS - 1:
-                transpose_chunk(c)
+            if 0 < c <= EARLY_CHUNKS:
+                transpose_chunk(c - 1)
+        transpose_chunk(EARLY_CHUNKS)
+        transpose_chunk(EARLY_CHUNKS + 1)
+        nc.vector.reduce_sum(out=scalar_part[:, 1:2], in_=squares[:], axis=mybir.AxisListType.X)
 
         moments_part = small.tile([P, 2], F32, name="moments_part")
         nc.vector.bn_aggr(out=moments_part[:], in_=stats[:].rearrange("p k s -> p (k s)"))
@@ -179,7 +199,8 @@ def tile_generator_pa_t_kernel(tc, x, U, C_words, C_scales, beta, gamma, bn_bias
         nc.vector.tensor_copy(out=sums_part[:, 0:1], in_=column_sums[:])
         quantise_u(0)
         total = s_banks.tile([P, 2], F32, name="total", tag="s")
-        nc.tensor.matmul(out=total[:], lhsT=weigh_mean[:], rhs=moments_part[:], start=True, stop=False)
+        nc.tensor.matmul(out=total[:], lhsT=weigh_sum[:], rhs=scalar_part[:], start=True, stop=False)
+        nc.tensor.matmul(out=total[:], lhsT=weigh_mean[:], rhs=moments_part[:], start=False, stop=False)
         nc.tensor.matmul(out=total[:], lhsT=weigh_sum[:], rhs=sums_part[:], start=False, stop=True)
         moments = small.tile([P, 2], F32, name="moments")
         nc.vector.tensor_copy(out=moments[:], in_=total[:])
@@ -192,7 +213,7 @@ def tile_generator_pa_t_kernel(tc, x, U, C_words, C_scales, beta, gamma, bn_bias
         nc.scalar.activation(
             out=rough[:], in_=minus_var[:], func=ACT.Abs_reciprocal_sqrt, scale=-1.0, bias=EPS
         )
-        transpose_chunk(X_CHUNKS - 1)
+        regroup_u(DEGREE - 1, True)
         minus_half_v = small.tile([P, 1], F32, name="minus_half_v")
         nc.vector.tensor_scalar(
             out=minus_half_v[:], in0=minus_var[:], scalar1=0.5, scalar2=-0.5 * EPS, op0=ALU.mult, op1=ALU.add
@@ -235,9 +256,9 @@ def tile_generator_pa_t_kernel(tc, x, U, C_words, C_scales, beta, gamma, bn_bias
         o_psum = {}
         o_sb = {}
 
-        def first_stage(i):
+        def first_stage(i, degrees):
             codes, scales = z_operand[i]
-            for n in range(DEGREE):
+            for n in degrees:
                 if n % 2 == 0:
                     bank = s_banks.tile([P, PACK, P], F32, name="s", tag="s")
                 else:
@@ -253,15 +274,19 @@ def tile_generator_pa_t_kernel(tc, x, U, C_words, C_scales, beta, gamma, bn_bias
                         stop=True,
                     )
                 t_psum[i, n] = bank[:].rearrange("p j b -> p b j")
-            left[i] = work.tile([P, P, PACK], F32, name="left")
-            right[i] = work.tile([P, P, PACK], F32, name="right")
-            nc.scalar.copy(out=left[i][:], in_=t_psum[i, 0])
-            nc.scalar.activation(out=right[i][:], in_=t_psum[i, 2], func=ACT.Identity, bias=1.0)
+                if n == 0:
+                    left[i] = work.tile([P, P, PACK], F32, name="left")
+                    nc.scalar.copy(out=left[i][:], in_=t_psum[i, 0])
+                if n == 2:
+                    right[i] = work.tile([P, P, PACK], F32, name="right")
+                    nc.scalar.activation(out=right[i][:], in_=t_psum[i, 2], func=ACT.Identity, bias=1.0)
 
-        def multiply_factors(i):
+        def multiply_left(i):
             nc.vector.scalar_tensor_tensor(
                 out=left[i][:], in0=t_psum[i, 1], scalar=1.0, in1=left[i][:], op0=ALU.add, op1=ALU.mult
             )
+
+        def multiply_right(i):
             nc.vector.scalar_tensor_tensor(
                 out=right[i][:], in0=t_psum[i, 3], scalar=1.0, in1=right[i][:], op0=ALU.add, op1=ALU.mult
             )
@@ -305,31 +330,53 @@ def tile_generator_pa_t_kernel(tc, x, U, C_words, C_scales, beta, gamma, bn_bias
             nc.vector.tensor_tensor(
                 out=o_sb[i // 2][:, i % 2, :], in0=o_psum[i][:], in1=beta_bc[:], op=ALU.add
             )
-            if i % 2 == 1:
+            if i >= BLOCKS - 2:
+                nc.sync.dma_start(out=out_view[:, i, :], in_=o_sb[i // 2][:, i % 2, :])
+            elif i % 2 == 1:
                 nc.sync.dma_start(out=out_view[:, i - 1 : i + 1, :], in_=o_sb[i // 2][:])
 
         z_first = keep.tile([P, Z_AHEAD, P * PACK], BF16, name="z_first", align_bytes=64)
-        normalise(True, z_first[:], 0, Z_AHEAD)
-        nc.vector.quantize_mx(
-            out=z_codes[:].rearrange("p i b -> p (i b)").bitcast(FP8X4),
-            scales=z_scales[:].rearrange("p i b -> p (i b)"),
-            in_=z_first[:].rearrange("p i e -> p (i e)"),
-        )
-        for i in range(Z_AHEAD):
-            z_operand[i] = z_codes[:, i, :], z_scales[:, i, :]
+
+        def quantise_first_z(first, count):
+            blocks = slice(first, first + count)
+            nc.vector.quantize_mx(
+                out=z_codes[:, blocks].rearrange("p i b -> p (i b)").bitcast(FP8X4),
+                scales=z_scales[:, blocks].rearrange("p i b -> p (i b)"),
+                in_=z_first[:, blocks].rearrange("p i e -> p (i e)"),
+            )
+            for i in range(first, first + count):
+                z_operand[i] = z_codes[:, i, :], z_scales[:, i, :]
+
+        normalise(True, z_first[:, 0:1], 0, 1)
+        quantise_first_z(0, 1)
+        first_stage(0, (0, 1))
+        normalise(True, z_first[:, 1:], 1, Z_AHEAD - 1)
+        quantise_first_z(1, Z_AHEAD - 1)
+        first_stage(1, (0, 1))
         quantise_u(2)
+        first_stage(0, (2,))
+        multiply_left(0)
         quantise_u(3)
-        first_stage(0)
-        for i in range(BLOCKS + OUT_LAG):
-            if i < BLOCKS:
-                multiply_factors(i)
-            if 0 <= i - QUANT_LAG < BLOCKS:
+        first_stage(0, (3,))
+        first_stage(1, (2, 3))
+        multiply_right(0)
+        for i in range(BLOCKS + OUT_LAG - 1):
+            if 0 < i < BLOCKS:
+                multiply_left(i)
+                multiply_right(i)
+            if 0 <= i - QUANT_LAG < BLOCKS - 1:
                 quantise(i - QUANT_LAG)
-            if i + 1 < BLOCKS:
-                first_stage(i + 1)
-            if 0 <= i - W_LAG < BLOCKS:
+            if 1 < i + 1 < BLOCKS:
+                first_stage(i + 1, range(DEGREE))
+            if 0 <= i - W_LAG < BLOCKS - 1:
                 second_stage(i - W_LAG)
+            late, rest = divmod(i - LATE_ROUND, LATE_STEP)
+            if rest == 0 and 0 <= late < LATE_PAIRS:
+                transpose_pair(BLOCKS // 2 - LATE_PAIRS + late)
             if i + Z_AHEAD < BLOCKS:
                 normalise(False, hz[i][:, 1:2, :], i + Z_AHEAD, 1)
             if 0 <= i - OUT_LAG:
                 add_beta_and_store(i - OUT_LAG)
+        quantise(BLOCKS - 1)
+        second_stage(BLOCKS - 1)
+        add_beta_and_store(BLOCKS - 1)

@@ -20,14 +20,16 @@ BLOCKS = BATCH // P
 EPS = 1e-5
 X_CHUNK = 4
 X_CHUNKS = BLOCKS // X_CHUNK
-SQUARE_CHUNKS = 7
+VECTOR_BLOCKS = range(0, BLOCKS - 2 * X_CHUNK, 2)
+GRAM_BLOCKS = [*range(1, BLOCKS - 2 * X_CHUNK, 4), *range(BLOCKS - 2 * X_CHUNK, BLOCKS - X_CHUNK - 1), BLOCKS - 4]
+SQUARE_BLOCKS = [*range(3, BLOCKS - X_CHUNK, 4), BLOCKS - 3, BLOCKS - 2]
 Z_AHEAD = 5
 QUANT_LAG = 2
 W_LAG = 3
-OUT_LAG = 4
+OUT_LAG = 3
 EARLY_CHUNKS = 4
-LATE_PAIRS = 4
-LATE_ROUND = 2
+LATE_PAIRS = (X_CHUNKS - EARLY_CHUNKS) * X_CHUNK // 2
+LATE_ROUND = 1
 LATE_STEP = 3
 
 FLOPS = 2 * BATCH * PIXELS * RANK * (DEGREE + 1)
@@ -61,16 +63,15 @@ def tile_generator_pa_t_kernel(tc, x, U, C_words, C_scales, beta, gamma, bn_bias
                 in_=U[n].rearrange("(u p e) r -> p u e r", u=2, e=2),
             )
 
-        for c in range(X_CHUNKS):
-            pieces = 2 if c == X_CHUNKS - 1 else 1
-            for k in range(pieces):
-                size = X_CHUNK // pieces
-                blocks = slice(c * X_CHUNK + k * size, c * X_CHUNK + (k + 1) * size)
-                nc.sync.dma_start(out=x_sb[:, blocks, :], in_=x_view[:, blocks, :])
-            if c == 3:
-                load_u(0)
-        for n in range(1, DEGREE):
-            load_u(n)
+        pieces = [(first, X_CHUNK) for first in range(0, BLOCKS - X_CHUNK, X_CHUNK)]
+        pieces += [(BLOCKS - 4, 2), (BLOCKS - 2, 1), (BLOCKS - 1, 1)]
+        for k, (first, count) in enumerate(pieces):
+            blocks = slice(first, first + count)
+            nc.sync.dma_start(out=x_sb[:, blocks, :], in_=x_view[:, blocks, :])
+            if k in (1, 3):
+                load_u(k // 2)
+        load_u(2)
+        load_u(3)
         w_codes = keep.tile([P, PIXELS], U32, name="w_codes", align_bytes=64)
         w_scales = keep.tile([P, PIXELS], U8, name="w_scales", align_bytes=64)
         nc.vector.memset(w_scales[:].bitcast(I32), 0)
@@ -91,7 +92,7 @@ def tile_generator_pa_t_kernel(tc, x, U, C_words, C_scales, beta, gamma, bn_bias
         ones = keep.tile([P, 1], BF16, name="ones")
         nc.vector.memset(ones[:], 1.0)
         weigh_mean = keep.tile([P, P], F32, name="weigh_mean")
-        nc.vector.memset(weigh_mean[:], 1.0 / (2 * P))
+        nc.vector.memset(weigh_mean[:], len(VECTOR_BLOCKS) / BLOCKS / P)
         weigh_sum = keep.tile([P, P], F32, name="weigh_sum")
         nc.vector.memset(weigh_sum[:], 1.0 / (BATCH * PIXELS))
         one = small.tile([P, 1], F32, name="one")
@@ -142,84 +143,104 @@ def tile_generator_pa_t_kernel(tc, x, U, C_words, C_scales, beta, gamma, bn_bias
         for n in range(DEGREE - 1):
             regroup_u(n, False)
 
-        stats = small.tile([P, BLOCKS // 2, 6], F32, name="stats")
-        squares = small.tile([P, SQUARE_CHUNKS], F32, name="squares")
-        unread_x = keep.tile([P, SQUARE_CHUNKS, PIXELS], BF16, name="unread_x")
-        scalar_part = small.tile([P, 2], F32, name="scalar_part")
-        nc.vector.memset(scalar_part[:, 0:1], 0.0)
+        stats = small.tile([P, len(VECTOR_BLOCKS), 6], F32, name="stats")
+        squares = small.tile([P, len(SQUARE_BLOCKS) + 2], F32, name="squares")
+        unread_x = keep.tile([P, len(SQUARE_BLOCKS) + 1, PIXELS], BF16, name="unread_x")
+        unread_gram = keep.tile([P, P], F32, name="unread_gram")
+        moments_part = small.tile([P, 2], F32, name="moments_part")
+        sums_part = small.tile([P, 2], F32, name="sums_part")
         gram = o_banks.tile([P, P], F32, name="gram", tag="o")
         column_sums = o_banks.tile([P, 1], F32, name="column_sums", tag="o")
-        for c in range(X_CHUNKS):
-            for i in range(c * X_CHUNK, (c + 1) * X_CHUNK):
-                if i % 2 == 0:
-                    nc.vector.bn_stats(out=stats[:, i // 2, :], in_=x_sb[:, i, :])
-                    continue
-                by_scalar = c < SQUARE_CHUNKS and i % X_CHUNK == X_CHUNK - 1
-                if by_scalar:
-                    nc.scalar.activation(
-                        out=unread_x[:, c],
-                        in_=x_sb[:, i, :],
-                        func=ACT.Square,
-                        accum_out=squares[:, c : c + 1],
-                    )
-                for q in range(PIXELS // P):
-                    columns = x_sb[:, i, q * P : (q + 1) * P]
-                    first = i == 1 and q == 0
-                    last = i == BLOCKS - 1 and q == PIXELS // P - 1
-                    if not by_scalar:
-                        nc.tensor.matmul(out=gram[:], lhsT=columns, rhs=columns, start=first, stop=last)
-                    nc.tensor.matmul(out=column_sums[:], lhsT=columns, rhs=ones[:], start=first, stop=last)
-            if 0 < c <= EARLY_CHUNKS:
-                transpose_chunk(c - 1)
-        transpose_chunk(EARLY_CHUNKS)
-        transpose_chunk(EARLY_CHUNKS + 1)
-        nc.vector.reduce_sum(out=scalar_part[:, 1:2], in_=squares[:], axis=mybir.AxisListType.X)
+        sum_blocks = [i for i in range(BLOCKS) if i not in VECTOR_BLOCKS]
 
-        moments_part = small.tile([P, 2], F32, name="moments_part")
-        nc.vector.bn_aggr(out=moments_part[:], in_=stats[:].rearrange("p k s -> p (k s)"))
+        def column_of(i, q):
+            return x_sb[:, i, q * P : (q + 1) * P]
+
+        for i in range(BLOCKS):
+            if i in VECTOR_BLOCKS:
+                nc.vector.bn_stats(out=stats[:, VECTOR_BLOCKS.index(i), :], in_=x_sb[:, i, :])
+            if i in SQUARE_BLOCKS:
+                k = SQUARE_BLOCKS.index(i)
+                nc.scalar.activation(
+                    out=unread_x[:, k], in_=x_sb[:, i, :], func=ACT.Square, accum_out=squares[:, k : k + 1]
+                )
+            for q in range(PIXELS // P):
+                if i in GRAM_BLOCKS:
+                    nc.tensor.matmul(
+                        out=gram[:],
+                        lhsT=column_of(i, q),
+                        rhs=column_of(i, q),
+                        start=(i == GRAM_BLOCKS[0] and q == 0),
+                        stop=(i == GRAM_BLOCKS[-1] and q == PIXELS // P - 1),
+                    )
+                if i in sum_blocks:
+                    nc.tensor.matmul(
+                        out=column_sums[:],
+                        lhsT=column_of(i, q),
+                        rhs=ones[:],
+                        start=(i == sum_blocks[0] and q == 0),
+                        stop=(i == sum_blocks[-1] and q == PIXELS // P - 1),
+                    )
+            c, rest = divmod(i, X_CHUNK)
+            if rest == X_CHUNK - 1 and 0 < c < EARLY_CHUNKS:
+                transpose_chunk(c - 1)
+            if i == VECTOR_BLOCKS[-1]:
+                nc.vector.bn_aggr(out=moments_part[:], in_=stats[:].rearrange("p k s -> p (k s)"))
+                nc.vector.scalar_tensor_tensor(
+                    out=moments_part[:, 1:2],
+                    in0=moments_part[:, 0:1],
+                    scalar=moments_part[:, 0:1],
+                    in1=moments_part[:, 1:2],
+                    op0=ALU.mult,
+                    op1=ALU.add,
+                )
         nc.vector.scalar_tensor_tensor(
-            out=moments_part[:, 1:2],
-            in0=moments_part[:, 0:1],
-            scalar=moments_part[:, 0:1],
-            in1=moments_part[:, 1:2],
+            out=unread_x[:, len(SQUARE_BLOCKS)],
+            in0=x_sb[:, BLOCKS - 1, :],
+            scalar=1.0,
+            in1=x_sb[:, BLOCKS - 1, :],
             op0=ALU.mult,
-            op1=ALU.add,
+            op1=ALU.mult,
+            accum_out=squares[:, len(SQUARE_BLOCKS) + 1 :],
         )
-        sums_part = small.tile([P, 2], F32, name="sums_part")
-        unread = keep.tile([P, P], F32, name="unread")
         nc.vector.scalar_tensor_tensor(
-            out=unread[:],
+            out=unread_gram[:],
             in0=gram[:],
             scalar=1.0,
             in1=ident[:],
             op0=ALU.mult,
             op1=ALU.mult,
-            accum_out=sums_part[:, 1:2],
+            accum_out=squares[:, len(SQUARE_BLOCKS) : len(SQUARE_BLOCKS) + 1],
         )
-        nc.vector.tensor_copy(out=sums_part[:, 0:1], in_=column_sums[:])
+
+        nc.scalar.copy(out=sums_part[:, 0:1], in_=column_sums[:])
+        transpose_pair(EARLY_CHUNKS * X_CHUNK // 2 - 2)
+        nc.vector.reduce_sum(out=sums_part[:, 1:2], in_=squares[:], axis=mybir.AxisListType.X)
         quantise_u(0)
         total = s_banks.tile([P, 2], F32, name="total", tag="s")
-        nc.tensor.matmul(out=total[:], lhsT=weigh_sum[:], rhs=scalar_part[:], start=True, stop=False)
-        nc.tensor.matmul(out=total[:], lhsT=weigh_mean[:], rhs=moments_part[:], start=False, stop=False)
+        nc.tensor.matmul(out=total[:], lhsT=weigh_mean[:], rhs=moments_part[:], start=True, stop=False)
         nc.tensor.matmul(out=total[:], lhsT=weigh_sum[:], rhs=sums_part[:], start=False, stop=True)
-        moments = small.tile([P, 2], F32, name="moments")
-        nc.vector.tensor_copy(out=moments[:], in_=total[:])
-        mean = moments[:, 0:1]
         minus_var = small.tile([P, 1], F32, name="minus_var")
-        nc.vector.scalar_tensor_tensor(
-            out=minus_var[:], in0=mean, scalar=mean, in1=moments[:, 1:2], op0=ALU.mult, op1=ALU.subtract
+        nc.vector.tensor_scalar(
+            out=minus_var[:],
+            in0=total[:, 0:1],
+            scalar1=total[:, 0:1],
+            scalar2=total[:, 1:2],
+            op0=ALU.mult,
+            op1=ALU.subtract,
         )
         rough = small.tile([P, 1], F32, name="rough")
         nc.scalar.activation(
             out=rough[:], in_=minus_var[:], func=ACT.Abs_reciprocal_sqrt, scale=-1.0, bias=EPS
         )
+        transpose_pair(EARLY_CHUNKS * X_CHUNK // 2 - 1)
         regroup_u(DEGREE - 1, True)
         minus_half_v = small.tile([P, 1], F32, name="minus_half_v")
         nc.vector.tensor_scalar(
             out=minus_half_v[:], in0=minus_var[:], scalar1=0.5, scalar2=-0.5 * EPS, op0=ALU.mult, op1=ALU.add
         )
         minus_mean = small.tile([P, 1], F32, name="minus_mean")
-        nc.vector.tensor_scalar(out=minus_mean[:], in0=mean, scalar1=-1.0, scalar2=None, op0=ALU.mult)
+        nc.vector.tensor_scalar(out=minus_mean[:], in0=total[:, 0:1], scalar1=-1.0, scalar2=None, op0=ALU.mult)
         quantise_u(1)
         correction = small.tile([P, 1], F32, name="correction")
         nc.vector.tensor_scalar(
@@ -290,6 +311,8 @@ def tile_generator_pa_t_kernel(tc, x, U, C_words, C_scales, beta, gamma, bn_bias
             nc.vector.scalar_tensor_tensor(
                 out=right[i][:], in0=t_psum[i, 3], scalar=1.0, in1=right[i][:], op0=ALU.add, op1=ALU.mult
             )
+
+        def join(i):
             hz[i] = work.tile([P, 2, P * PACK], BF16, name="hz", align_bytes=64)
             nc.gpsimd.tensor_tensor(
                 out=hz[i][:, 0, :],
@@ -313,7 +336,12 @@ def tile_generator_pa_t_kernel(tc, x, U, C_words, C_scales, beta, gamma, bn_bias
 
         def second_stage(i):
             codes, scales = h_operand[i]
-            o_psum[i] = o_banks.tile([P, PIXELS], F32, name="o_psum", tag="o")
+            if i == BLOCKS - 2:
+                o_psum[i] = s_banks.tile([P, PIXELS], F32, name="o_psum", tag="s")
+            elif i == BLOCKS - 1:
+                o_psum[i] = v_banks.tile([P, PIXELS], F32, name="o_psum", tag="v")
+            else:
+                o_psum[i] = o_banks.tile([P, PIXELS], F32, name="o_psum", tag="o")
             nc.tensor.matmul_mx(
                 out=o_psum[i][:],
                 lhsT=codes.bitcast(FP8X4),
@@ -327,12 +355,14 @@ def tile_generator_pa_t_kernel(tc, x, U, C_words, C_scales, beta, gamma, bn_bias
         def add_beta_and_store(i):
             if i % 2 == 0:
                 o_sb[i // 2] = work.tile([P, 2, PIXELS], F32, name="o_sb")
-            nc.vector.tensor_tensor(
-                out=o_sb[i // 2][:, i % 2, :], in0=o_psum[i][:], in1=beta_bc[:], op=ALU.add
-            )
-            if i >= BLOCKS - 2:
-                nc.sync.dma_start(out=out_view[:, i, :], in_=o_sb[i // 2][:, i % 2, :])
-            elif i % 2 == 1:
+            halves = 2 if i == BLOCKS - 1 else 1
+            for k in range(halves):
+                columns = slice(k * PIXELS // halves, (k + 1) * PIXELS // halves)
+                o_block = o_sb[i // 2][:, i % 2, columns]
+                nc.vector.tensor_tensor(out=o_block, in0=o_psum[i][:, columns], in1=beta_bc[:, columns], op=ALU.add)
+                if i >= BLOCKS - 2:
+                    nc.sync.dma_start(out=out_view[:, i, columns], in_=o_block)
+            if i < BLOCKS - 2 and i % 2 == 1:
                 nc.sync.dma_start(out=out_view[:, i - 1 : i + 1, :], in_=o_sb[i // 2][:])
 
         z_first = keep.tile([P, Z_AHEAD, P * PACK], BF16, name="z_first", align_bytes=64)
@@ -351,32 +381,39 @@ def tile_generator_pa_t_kernel(tc, x, U, C_words, C_scales, beta, gamma, bn_bias
         quantise_first_z(0, 1)
         first_stage(0, (0, 1))
         normalise(True, z_first[:, 1:], 1, Z_AHEAD - 1)
-        quantise_first_z(1, Z_AHEAD - 1)
-        first_stage(1, (0, 1))
         quantise_u(2)
         first_stage(0, (2,))
-        multiply_left(0)
+        quantise_first_z(1, Z_AHEAD - 1)
+        first_stage(1, (0, 1))
         quantise_u(3)
         first_stage(0, (3,))
+        multiply_left(0)
         first_stage(1, (2, 3))
         multiply_right(0)
-        for i in range(BLOCKS + OUT_LAG - 1):
-            if 0 < i < BLOCKS:
+        join(0)
+        for i in range(BLOCKS):
+            if i > 0:
                 multiply_left(i)
                 multiply_right(i)
-            if 0 <= i - QUANT_LAG < BLOCKS - 1:
+                join(i)
+            if i >= QUANT_LAG:
                 quantise(i - QUANT_LAG)
-            if 1 < i + 1 < BLOCKS:
-                first_stage(i + 1, range(DEGREE))
-            if 0 <= i - W_LAG < BLOCKS - 1:
+            if i >= W_LAG:
                 second_stage(i - W_LAG)
+            if 0 < i < BLOCKS - 1:
+                first_stage(i + 1, range(DEGREE))
             late, rest = divmod(i - LATE_ROUND, LATE_STEP)
             if rest == 0 and 0 <= late < LATE_PAIRS:
                 transpose_pair(BLOCKS // 2 - LATE_PAIRS + late)
             if i + Z_AHEAD < BLOCKS:
                 normalise(False, hz[i][:, 1:2, :], i + Z_AHEAD, 1)
-            if 0 <= i - OUT_LAG:
+            if i >= OUT_LAG:
                 add_beta_and_store(i - OUT_LAG)
+        quantise(BLOCKS - 2)
+        for i in (BLOCKS - 3, BLOCKS - 2):
+            second_stage(i)
+        add_beta_and_store(BLOCKS - 3)
         quantise(BLOCKS - 1)
         second_stage(BLOCKS - 1)
+        add_beta_and_store(BLOCKS - 2)
         add_beta_and_store(BLOCKS - 1)

@@ -20,16 +20,20 @@ BLOCKS = BATCH // P
 EPS = 1e-5
 X_CHUNK = 4
 X_CHUNKS = BLOCKS // X_CHUNK
-VECTOR_BLOCKS = range(0, BLOCKS - 2 * X_CHUNK, 2)
-GRAM_BLOCKS = [*range(1, BLOCKS - 2 * X_CHUNK, 4), *range(BLOCKS - 2 * X_CHUNK, BLOCKS - X_CHUNK - 1), BLOCKS - 4]
+U_AFTER_CHUNK = (1, 3)
+VECTOR_BLOCKS = [
+    i for i in range(BLOCKS - 2 * X_CHUNK) if i % 2 == 0 or (i % X_CHUNK == 1 and i // X_CHUNK in U_AFTER_CHUNK)
+]
 SQUARE_BLOCKS = [*range(3, BLOCKS - X_CHUNK, 4), BLOCKS - 3, BLOCKS - 2]
+GRAM_BLOCKS = [i for i in range(BLOCKS - 1) if i not in VECTOR_BLOCKS and i not in SQUARE_BLOCKS]
+ONES = 64
 Z_AHEAD = 5
 QUANT_LAG = 2
 W_LAG = 3
 OUT_LAG = 3
 EARLY_CHUNKS = 4
 LATE_PAIRS = (X_CHUNKS - EARLY_CHUNKS) * X_CHUNK // 2
-LATE_ROUND = 1
+LATE_ROUND = 3
 LATE_STEP = 3
 
 FLOPS = 2 * BATCH * PIXELS * RANK * (DEGREE + 1)
@@ -68,8 +72,8 @@ def tile_generator_pa_t_kernel(tc, x, U, C_words, C_scales, beta, gamma, bn_bias
         for k, (first, count) in enumerate(pieces):
             blocks = slice(first, first + count)
             nc.sync.dma_start(out=x_sb[:, blocks, :], in_=x_view[:, blocks, :])
-            if k in (1, 3):
-                load_u(k // 2)
+            if k in U_AFTER_CHUNK:
+                load_u(U_AFTER_CHUNK.index(k))
         load_u(2)
         load_u(3)
         w_codes = keep.tile([P, PIXELS], U32, name="w_codes", align_bytes=64)
@@ -89,8 +93,13 @@ def tile_generator_pa_t_kernel(tc, x, U, C_words, C_scales, beta, gamma, bn_bias
 
         ident = keep.tile([P, P], F32, name="ident")
         make_identity(nc, ident[:])
-        ones = keep.tile([P, 1], BF16, name="ones")
+        ones = keep.tile([P, ONES], BF16, name="ones")
         nc.vector.memset(ones[:], 1.0)
+        three_halves = small.tile([P, 1], F32, name="three_halves")
+        nc.vector.memset(three_halves[:], 1.5)
+        gamma_bias = small.tile([P, 2], F32, name="gamma_bias")
+        nc.gpsimd.tensor_copy(out=gamma_bias[:, 0:1], in_=gamma_sb[:])
+        nc.gpsimd.tensor_copy(out=gamma_bias[:, 1:2], in_=bias_sb[:])
         weigh_mean = keep.tile([P, P], F32, name="weigh_mean")
         nc.vector.memset(weigh_mean[:], len(VECTOR_BLOCKS) / BLOCKS / P)
         weigh_sum = keep.tile([P, P], F32, name="weigh_sum")
@@ -150,7 +159,7 @@ def tile_generator_pa_t_kernel(tc, x, U, C_words, C_scales, beta, gamma, bn_bias
         moments_part = small.tile([P, 2], F32, name="moments_part")
         sums_part = small.tile([P, 2], F32, name="sums_part")
         gram = o_banks.tile([P, P], F32, name="gram", tag="o")
-        column_sums = o_banks.tile([P, 1], F32, name="column_sums", tag="o")
+        column_sums = o_banks.tile([P, ONES], F32, name="column_sums", tag="o")
         sum_blocks = [i for i in range(BLOCKS) if i not in VECTOR_BLOCKS]
 
         def column_of(i, q):
@@ -194,6 +203,8 @@ def tile_generator_pa_t_kernel(tc, x, U, C_words, C_scales, beta, gamma, bn_bias
                     op0=ALU.mult,
                     op1=ALU.add,
                 )
+                quantise_u(0)
+                quantise_u(1)
         nc.vector.scalar_tensor_tensor(
             out=unread_x[:, len(SQUARE_BLOCKS)],
             in0=x_sb[:, BLOCKS - 1, :],
@@ -213,10 +224,9 @@ def tile_generator_pa_t_kernel(tc, x, U, C_words, C_scales, beta, gamma, bn_bias
             accum_out=squares[:, len(SQUARE_BLOCKS) : len(SQUARE_BLOCKS) + 1],
         )
 
-        nc.scalar.copy(out=sums_part[:, 0:1], in_=column_sums[:])
+        nc.scalar.copy(out=sums_part[:, 0:1], in_=column_sums[:, 0:1])
         transpose_pair(EARLY_CHUNKS * X_CHUNK // 2 - 2)
         nc.vector.reduce_sum(out=sums_part[:, 1:2], in_=squares[:], axis=mybir.AxisListType.X)
-        quantise_u(0)
         total = s_banks.tile([P, 2], F32, name="total", tag="s")
         nc.tensor.matmul(out=total[:], lhsT=weigh_mean[:], rhs=moments_part[:], start=True, stop=False)
         nc.tensor.matmul(out=total[:], lhsT=weigh_sum[:], rhs=sums_part[:], start=False, stop=True)
@@ -241,20 +251,21 @@ def tile_generator_pa_t_kernel(tc, x, U, C_words, C_scales, beta, gamma, bn_bias
         )
         minus_mean = small.tile([P, 1], F32, name="minus_mean")
         nc.vector.tensor_scalar(out=minus_mean[:], in0=total[:, 0:1], scalar1=-1.0, scalar2=None, op0=ALU.mult)
-        quantise_u(1)
         correction = small.tile([P, 1], F32, name="correction")
         nc.vector.tensor_scalar(
             out=correction[:], in0=rough[:], scalar1=rough[:], scalar2=minus_half_v[:], op0=ALU.mult, op1=ALU.mult
         )
         rough_gamma = small.tile([P, 1], F32, name="rough_gamma")
-        nc.vector.tensor_tensor(out=rough_gamma[:], in0=rough[:], in1=gamma_sb[:], op=ALU.mult)
+        nc.vector.tensor_scalar(
+            out=rough_gamma[:], in0=rough[:], scalar1=gamma_bias[:, 0:1], scalar2=None, op0=ALU.mult
+        )
         scale_a = small.tile([P, 1], F32, name="scale_a")
         shift_b = small.tile([P, 1], F32, name="shift_b")
-        nc.vector.scalar_tensor_tensor(
-            out=scale_a[:], in0=correction[:], scalar=1.5, in1=rough_gamma[:], op0=ALU.add, op1=ALU.mult
+        nc.vector.tensor_scalar(
+            out=scale_a[:], in0=correction[:], scalar1=three_halves[:], scalar2=rough_gamma[:], op0=ALU.add, op1=ALU.mult
         )
-        nc.vector.scalar_tensor_tensor(
-            out=shift_b[:], in0=minus_mean[:], scalar=scale_a[:], in1=bias_sb[:], op0=ALU.mult, op1=ALU.add
+        nc.vector.tensor_scalar(
+            out=shift_b[:], in0=minus_mean[:], scalar1=scale_a[:], scalar2=gamma_bias[:, 1:2], op0=ALU.mult, op1=ALU.add
         )
 
         def normalise(engine_is_vector, z_blocks, first, count):

import concourse.mybir as mybir
from concourse.masks import make_identity

F32 = mybir.dt.float32
BF16 = mybir.dt.bfloat16
I32 = mybir.dt.int32
U32 = mybir.dt.uint32
U8 = mybir.dt.uint8
FP8X4 = mybir.dt.float8_e4m3fn_x4
ALU = mybir.AluOpType
ACT = mybir.ActivationFunctionType

P = 128
PACK = 4
DEGREE = 4
BATCH = 4096
PIXELS = 512
RANK = 512
BLOCKS = BATCH // P
EPS = 1e-5
X_CHUNK = 4
X_CHUNKS = BLOCKS // X_CHUNK
U_AFTER_CHUNK = (1, 3)
VECTOR_BLOCKS = [
    i for i in range(BLOCKS - 2 * X_CHUNK) if i % 2 == 0 or (i % X_CHUNK == 1 and i // X_CHUNK in U_AFTER_CHUNK)
]
SQUARE_BLOCKS = [*range(3, BLOCKS - X_CHUNK, 4), BLOCKS - 3, BLOCKS - 2]
GRAM_BLOCKS = [i for i in range(BLOCKS - 1) if i not in VECTOR_BLOCKS and i not in SQUARE_BLOCKS]
ONES = 64
Z_AHEAD = 5
QUANT_LAG = 2
W_LAG = 3
OUT_LAG = 3
EARLY_CHUNKS = 4
LATE_PAIRS = (X_CHUNKS - EARLY_CHUNKS) * X_CHUNK // 2
LATE_ROUND = 3
LATE_STEP = 3

FLOPS = 2 * BATCH * PIXELS * RANK * (DEGREE + 1)


def tile_generator_pa_t_kernel(tc, x, U, C_words, C_scales, beta, gamma, bn_bias, out):
    nc = tc.nc
    x_view = x.rearrange("(p i) c h w -> p i (c h w)", i=BLOCKS)
    out_view = out.rearrange("(p i) c h w -> p i (c h w)", i=BLOCKS)

    with (
        tc.tile_pool(name="keep", bufs=1) as keep,
        tc.tile_pool(name="small", bufs=1) as small,
        tc.tile_pool(name="work", bufs=4) as work,
        tc.tile_pool(name="codes", bufs=8) as codes_pool,
        tc.psum_pool(name="s_banks", bufs=3) as s_banks,
        tc.psum_pool(name="v_banks", bufs=3) as v_banks,
        tc.psum_pool(name="o_banks", bufs=2) as o_banks,
        tc.manual_schedule(),
    ):
        x_sb = keep.tile([P, BLOCKS, PIXELS], BF16, name="x_sb")
        u_raw = keep.tile([P, DEGREE, PACK, RANK], BF16, name="u_raw")
        gamma_sb = small.tile([P, 1], BF16, name="gamma_sb")
        bias_sb = small.tile([P, 1], BF16, name="bias_sb")
        nc.scalar.dma_start(out=gamma_sb[:], in_=gamma.partition_broadcast(P))
        nc.scalar.dma_start(out=bias_sb[:], in_=bn_bias.partition_broadcast(P))

        def load_u(n):
            nc.sync.dma_start(
                out=u_raw[:, n].rearrange("p (u e) r -> p u e r", u=2),
                in_=U[n].rearrange("(u p e) r -> p u e r", u=2, e=2),
            )

        pieces = [(first, X_CHUNK) for first in range(0, BLOCKS - X_CHUNK, X_CHUNK)]
        pieces += [(BLOCKS - 4, 2), (BLOCKS - 2, 1), (BLOCKS - 1, 1)]
        for k, (first, count) in enumerate(pieces):
            blocks = slice(first, first + count)
            nc.sync.dma_start(out=x_sb[:, blocks, :], in_=x_view[:, blocks, :])
            if k in U_AFTER_CHUNK:
                load_u(U_AFTER_CHUNK.index(k))
        load_u(2)
        load_u(3)
        w_codes = keep.tile([P, PIXELS], U32, name="w_codes", align_bytes=64)
        w_scales = keep.tile([P, PIXELS], U8, name="w_scales", align_bytes=64)
        nc.vector.memset(w_scales[:].bitcast(I32), 0)
        nc.sync.dma_start(
            out=w_codes[:].bitcast(I32),
            in_=C_words[0].rearrange("p n t -> p (n t)").bitcast(I32),
        )
        for quadrant in range(4):
            nc.sync.dma_start(
                out=w_scales[32 * quadrant : 32 * quadrant + 4, :].bitcast(I32),
                in_=C_scales[0, 4 * quadrant : 4 * quadrant + 4, :].bitcast(I32),
            )
        beta_bc = keep.tile([P, PIXELS], BF16, name="beta_bc")
        nc.sync.dma_start(out=beta_bc[:], in_=beta.partition_broadcast(P))

        ident = keep.tile([P, P], F32, name="ident")
        make_identity(nc, ident[:])
        ones = keep.tile([P, ONES], BF16, name="ones")
        nc.vector.memset(ones[:], 1.0)
        three_halves = small.tile([P, 1], F32, name="three_halves")
        nc.vector.memset(three_halves[:], 1.5)
        gamma_bias = small.tile([P, 2], F32, name="gamma_bias")
        nc.gpsimd.tensor_copy(out=gamma_bias[:, 0:1], in_=gamma_sb[:])
        nc.gpsimd.tensor_copy(out=gamma_bias[:, 1:2], in_=bias_sb[:])
        weigh_mean = keep.tile([P, P], F32, name="weigh_mean")
        nc.vector.memset(weigh_mean[:], len(VECTOR_BLOCKS) / BLOCKS / P)
        weigh_sum = keep.tile([P, P], F32, name="weigh_sum")
        nc.vector.memset(weigh_sum[:], 1.0 / (BATCH * PIXELS))
        one = small.tile([P, 1], F32, name="one")
        nc.vector.memset(one[:], 1.0)
        warm = small.tile([P, 1], F32, name="warm")
        nc.scalar.activation(out=warm[:], in_=one[:], func=ACT.Abs_reciprocal_sqrt)

        xT = keep.tile([P, BLOCKS, P, PACK], BF16, name="xT", align_bytes=64)
        z_codes = keep.tile([P, Z_AHEAD, P], U32, name="z_codes", align_bytes=64)
        z_scales = keep.tile([P, Z_AHEAD, P], U8, name="z_scales", align_bytes=64)
        u_codes = keep.tile([P, DEGREE, PACK, P], U32, name="u_codes", align_bytes=64)
        u_scales = keep.tile([P, DEGREE, PACK, P], U8, name="u_scales", align_bytes=64)

        def transpose_pair(pair):
            xt = v_banks.tile([P, 2, 2, P], F32, name="xt", tag="v")
            for k in range(2):
                words = x_sb[:, 2 * pair + k, :].bitcast(F32)
                for u in range(2):
                    nc.tensor.transpose(xt[:, k, u, :], words[:, u * P : (u + 1) * P], ident[:])
            nc.scalar.copy(
                out=xT[:, 2 * pair : 2 * pair + 2, :, :].bitcast(F32),
                in_=xt[:].rearrange("p k u b -> p k b u"),
            )

        def transpose_chunk(c):
            for pair in range(c * X_CHUNK // 2, (c + 1) * X_CHUNK // 2):
                transpose_pair(pair)

        u_grouped = {}

        def regroup_u(n, on_scalar):
            u_grouped[n] = keep.tile([P, PACK, P, PACK], BF16, name="u_grouped%d" % n, align_bytes=64)
            raw = u_raw[:, n].rearrange("p t (q j) -> p j q t", j=PACK)
            if on_scalar:
                nc.scalar.copy(out=u_grouped[n][:], in_=raw)
            else:
                nc.gpsimd.tensor_scalar(
                    out=u_grouped[n][:], in0=raw, scalar1=1.0, scalar2=0.0, op0=ALU.mult, op1=ALU.add
                )

        def quantise_u(n):
            nc.vector.quantize_mx(
                out=u_codes[:, n].rearrange("p j q -> p (j q)").bitcast(FP8X4),
                scales=u_scales[:, n].rearrange("p j q -> p (j q)"),
                in_=u_grouped[n][:].rearrange("p j q t -> p (j q t)"),
            )

        for n in range(DEGREE - 1):
            regroup_u(n, False)

        stats = small.tile([P, len(VECTOR_BLOCKS), 6], F32, name="stats")
        squares = small.tile([P, len(SQUARE_BLOCKS) + 2], F32, name="squares")
        unread_x = keep.tile([P, len(SQUARE_BLOCKS) + 1, PIXELS], BF16, name="unread_x")
        unread_gram = keep.tile([P, P], F32, name="unread_gram")
        moments_part = small.tile([P, 2], F32, name="moments_part")
        sums_part = small.tile([P, 2], F32, name="sums_part")
        gram = o_banks.tile([P, P], F32, name="gram", tag="o")
        column_sums = o_banks.tile([P, ONES], F32, name="column_sums", tag="o")
        sum_blocks = [i for i in range(BLOCKS) if i not in VECTOR_BLOCKS]

        def column_of(i, q):
            return x_sb[:, i, q * P : (q + 1) * P]

        for i in range(BLOCKS):
            if i in VECTOR_BLOCKS:
                nc.vector.bn_stats(out=stats[:, VECTOR_BLOCKS.index(i), :], in_=x_sb[:, i, :])
            if i in SQUARE_BLOCKS:
                k = SQUARE_BLOCKS.index(i)
                nc.scalar.activation(
                    out=unread_x[:, k], in_=x_sb[:, i, :], func=ACT.Square, accum_out=squares[:, k : k + 1]
                )
            for q in range(PIXELS // P):
                if i in GRAM_BLOCKS:
                    nc.tensor.matmul(
                        out=gram[:],
                        lhsT=column_of(i, q),
                        rhs=column_of(i, q),
                        start=(i == GRAM_BLOCKS[0] and q == 0),
                        stop=(i == GRAM_BLOCKS[-1] and q == PIXELS // P - 1),
                    )
                if i in sum_blocks:
                    nc.tensor.matmul(
                        out=column_sums[:],
                        lhsT=column_of(i, q),
                        rhs=ones[:],
                        start=(i == sum_blocks[0] and q == 0),
                        stop=(i == sum_blocks[-1] and q == PIXELS // P - 1),
                    )
            c, rest = divmod(i, X_CHUNK)
            if rest == X_CHUNK - 1 and 0 < c < EARLY_CHUNKS:
                transpose_chunk(c - 1)
            if i == VECTOR_BLOCKS[-1]:
                nc.vector.bn_aggr(out=moments_part[:], in_=stats[:].rearrange("p k s -> p (k s)"))
                nc.vector.scalar_tensor_tensor(
                    out=moments_part[:, 1:2],
                    in0=moments_part[:, 0:1],
                    scalar=moments_part[:, 0:1],
                    in1=moments_part[:, 1:2],
                    op0=ALU.mult,
                    op1=ALU.add,
                )
                quantise_u(0)
                quantise_u(1)
        nc.vector.scalar_tensor_tensor(
            out=unread_x[:, len(SQUARE_BLOCKS)],
            in0=x_sb[:, BLOCKS - 1, :],
            scalar=1.0,
            in1=x_sb[:, BLOCKS - 1, :],
            op0=ALU.mult,
            op1=ALU.mult,
            accum_out=squares[:, len(SQUARE_BLOCKS) + 1 :],
        )
        nc.vector.scalar_tensor_tensor(
            out=unread_gram[:],
            in0=gram[:],
            scalar=1.0,
            in1=ident[:],
            op0=ALU.mult,
            op1=ALU.mult,
            accum_out=squares[:, len(SQUARE_BLOCKS) : len(SQUARE_BLOCKS) + 1],
        )

        nc.scalar.copy(out=sums_part[:, 0:1], in_=column_sums[:, 0:1])
        transpose_pair(EARLY_CHUNKS * X_CHUNK // 2 - 2)
        nc.vector.reduce_sum(out=sums_part[:, 1:2], in_=squares[:], axis=mybir.AxisListType.X)
        total = s_banks.tile([P, 2], F32, name="total", tag="s")
        nc.tensor.matmul(out=total[:], lhsT=weigh_mean[:], rhs=moments_part[:], start=True, stop=False)
        nc.tensor.matmul(out=total[:], lhsT=weigh_sum[:], rhs=sums_part[:], start=False, stop=True)
        minus_var = small.tile([P, 1], F32, name="minus_var")
        nc.vector.tensor_scalar(
            out=minus_var[:],
            in0=total[:, 0:1],
            scalar1=total[:, 0:1],
            scalar2=total[:, 1:2],
            op0=ALU.mult,
            op1=ALU.subtract,
        )
        rough = small.tile([P, 1], F32, name="rough")
        nc.scalar.activation(
            out=rough[:], in_=minus_var[:], func=ACT.Abs_reciprocal_sqrt, scale=-1.0, bias=EPS
        )
        transpose_pair(EARLY_CHUNKS * X_CHUNK // 2 - 1)
        regroup_u(DEGREE - 1, True)
        minus_half_v = small.tile([P, 1], F32, name="minus_half_v")
        nc.vector.tensor_scalar(
            out=minus_half_v[:], in0=minus_var[:], scalar1=0.5, scalar2=-0.5 * EPS, op0=ALU.mult, op1=ALU.add
        )
        minus_mean = small.tile([P, 1], F32, name="minus_mean")
        nc.vector.tensor_scalar(out=minus_mean[:], in0=total[:, 0:1], scalar1=-1.0, scalar2=None, op0=ALU.mult)
        correction = small.tile([P, 1], F32, name="correction")
        nc.vector.tensor_scalar(
            out=correction[:], in0=rough[:], scalar1=rough[:], scalar2=minus_half_v[:], op0=ALU.mult, op1=ALU.mult
        )
        rough_gamma = small.tile([P, 1], F32, name="rough_gamma")
        nc.vector.tensor_scalar(
            out=rough_gamma[:], in0=rough[:], scalar1=gamma_bias[:, 0:1], scalar2=None, op0=ALU.mult
        )
        scale_a = small.tile([P, 1], F32, name="scale_a")
        shift_b = small.tile([P, 1], F32, name="shift_b")
        nc.vector.tensor_scalar(
            out=scale_a[:], in0=correction[:], scalar1=three_halves[:], scalar2=rough_gamma[:], op0=ALU.add, op1=ALU.mult
        )
        nc.vector.tensor_scalar(
            out=shift_b[:], in0=minus_mean[:], scalar1=scale_a[:], scalar2=gamma_bias[:, 1:2], op0=ALU.mult, op1=ALU.add
        )

        def normalise(engine_is_vector, z_blocks, first, count):
            x_blocks = xT[:, first : first + count].rearrange("p i b t -> p i (b t)")
            if engine_is_vector:
                nc.vector.tensor_scalar(
                    out=z_blocks, in0=x_blocks, scalar1=scale_a[:], scalar2=shift_b[:], op0=ALU.mult, op1=ALU.add
                )
            else:
                nc.scalar.activation(
                    out=z_blocks, in_=x_blocks, func=ACT.Identity, scale=scale_a[:], bias=shift_b[:]
                )

        z_operand = {}
        t_psum = {}
        left = {}
        right = {}
        hz = {}
        h_operand = {}
        o_psum = {}
        o_sb = {}

        def first_stage(i, degrees):
            codes, scales = z_operand[i]
            for n in degrees:
                if n % 2 == 0:
                    bank = s_banks.tile([P, PACK, P], F32, name="s", tag="s")
                else:
                    bank = v_banks.tile([P, PACK, P], F32, name="v", tag="v")
                for j in range(PACK):
                    nc.tensor.matmul_mx(
                        out=bank[:, j, :],
                        lhsT=u_codes[:, n, j, :].bitcast(FP8X4),
                        lhsT_scale=u_scales[:, n, j, :],
                        rhs=codes.bitcast(FP8X4),
                        rhs_scale=scales,
                        start=True,
                        stop=True,
                    )
                t_psum[i, n] = bank[:].rearrange("p j b -> p b j")
                if n == 0:
                    left[i] = work.tile([P, P, PACK], F32, name="left")
                    nc.scalar.copy(out=left[i][:], in_=t_psum[i, 0])
                if n == 2:
                    right[i] = work.tile([P, P, PACK], F32, name="right")
                    nc.scalar.activation(out=right[i][:], in_=t_psum[i, 2], func=ACT.Identity, bias=1.0)

        def multiply_left(i):
            nc.vector.scalar_tensor_tensor(
                out=left[i][:], in0=t_psum[i, 1], scalar=1.0, in1=left[i][:], op0=ALU.add, op1=ALU.mult
            )

        def multiply_right(i):
            nc.vector.scalar_tensor_tensor(
                out=right[i][:], in0=t_psum[i, 3], scalar=1.0, in1=right[i][:], op0=ALU.add, op1=ALU.mult
            )

        def join(i):
            hz[i] = work.tile([P, 2, P * PACK], BF16, name="hz", align_bytes=64)
            nc.gpsimd.tensor_tensor(
                out=hz[i][:, 0, :],
                in0=left[i][:].rearrange("p b j -> p (b j)"),
                in1=right[i][:].rearrange("p b j -> p (b j)"),
                op=ALU.mult,
            )

        def quantise(i):
            count = 2 if i + Z_AHEAD < BLOCKS else 1
            codes = codes_pool.tile([P, 2, P], U32, name="hz_codes", align_bytes=64)
            scales = codes_pool.tile([P, 2, P], U8, name="hz_scales", align_bytes=64)
            nc.vector.quantize_mx(
                out=codes[:, :count].rearrange("p k b -> p (k b)").bitcast(FP8X4),
                scales=scales[:, :count].rearrange("p k b -> p (k b)"),
                in_=hz[i][:, :count].rearrange("p k e -> p (k e)"),
            )
            h_operand[i] = codes[:, 0, :], scales[:, 0, :]
            if count == 2:
                z_operand[i + Z_AHEAD] = codes[:, 1, :], scales[:, 1, :]

        def second_stage(i):
            codes, scales = h_operand[i]
            if i == BLOCKS - 2:
                o_psum[i] = s_banks.tile([P, PIXELS], F32, name="o_psum", tag="s")
            elif i == BLOCKS - 1:
                o_psum[i] = v_banks.tile([P, PIXELS], F32, name="o_psum", tag="v")
            else:
                o_psum[i] = o_banks.tile([P, PIXELS], F32, name="o_psum", tag="o")
            nc.tensor.matmul_mx(
                out=o_psum[i][:],
                lhsT=codes.bitcast(FP8X4),
                lhsT_scale=scales,
                rhs=w_codes[:].bitcast(FP8X4),
                rhs_scale=w_scales[:],
                start=True,
                stop=True,
            )

        def add_beta_and_store(i):
            if i % 2 == 0:
                o_sb[i // 2] = work.tile([P, 2, PIXELS], F32, name="o_sb")
            halves = 2 if i == BLOCKS - 1 else 1
            for k in range(halves):
                columns = slice(k * PIXELS // halves, (k + 1) * PIXELS // halves)
                o_block = o_sb[i // 2][:, i % 2, columns]
                nc.vector.tensor_tensor(out=o_block, in0=o_psum[i][:, columns], in1=beta_bc[:, columns], op=ALU.add)
                if i >= BLOCKS - 2:
                    nc.sync.dma_start(out=out_view[:, i, columns], in_=o_block)
            if i < BLOCKS - 2 and i % 2 == 1:
                nc.sync.dma_start(out=out_view[:, i - 1 : i + 1, :], in_=o_sb[i // 2][:])

        z_first = keep.tile([P, Z_AHEAD, P * PACK], BF16, name="z_first", align_bytes=64)

        def quantise_first_z(first, count):
            blocks = slice(first, first + count)
            nc.vector.quantize_mx(
                out=z_codes[:, blocks].rearrange("p i b -> p (i b)").bitcast(FP8X4),
                scales=z_scales[:, blocks].rearrange("p i b -> p (i b)"),
                in_=z_first[:, blocks].rearrange("p i e -> p (i e)"),
            )
            for i in range(first, first + count):
                z_operand[i] = z_codes[:, i, :], z_scales[:, i, :]

        normalise(True, z_first[:, 0:1], 0, 1)
        quantise_first_z(0, 1)
        first_stage(0, (0, 1))
        normalise(True, z_first[:, 1:], 1, Z_AHEAD - 1)
        quantise_u(2)
        first_stage(0, (2,))
        quantise_first_z(1, Z_AHEAD - 1)
        first_stage(1, (0, 1))
        quantise_u(3)
        first_stage(0, (3,))
        multiply_left(0)
        first_stage(1, (2, 3))
        multiply_right(0)
        join(0)
        for i in range(BLOCKS):
            if i > 0:
                multiply_left(i)
                multiply_right(i)
                join(i)
            if i >= QUANT_LAG:
                quantise(i - QUANT_LAG)
            if i >= W_LAG:
                second_stage(i - W_LAG)
            if 0 < i < BLOCKS - 1:
                first_stage(i + 1, range(DEGREE))
            late, rest = divmod(i - LATE_ROUND, LATE_STEP)
            if rest == 0 and 0 <= late < LATE_PAIRS:
                transpose_pair(BLOCKS // 2 - LATE_PAIRS + late)
            if i + Z_AHEAD < BLOCKS:
                normalise(False, hz[i][:, 1:2, :], i + Z_AHEAD, 1)
            if i >= OUT_LAG:
                add_beta_and_store(i - OUT_LAG)
        quantise(BLOCKS - 2)
        for i in (BLOCKS - 3, BLOCKS - 2):
            second_stage(i)
        add_beta_and_store(BLOCKS - 3)
        quantise(BLOCKS - 1)
        second_stage(BLOCKS - 1)
        add_beta_and_store(BLOCKS - 2)
        add_beta_and_store(BLOCKS - 1)
